import numpy as np
import ml_dtypes


def mxq(x, axis, fmt="e4m3"):
    dtype, down = {"e4m3": (ml_dtypes.float8_e4m3fn, 7), "e5m2": (ml_dtypes.float8_e5m2, 14)}[fmt]
    v = np.moveaxis(np.asarray(x, np.float32).astype(ml_dtypes.bfloat16).astype(np.float64), axis, -1)
    blocks = v.reshape(v.shape[:-1] + (-1, 32))
    amax = np.abs(blocks).max(-1, keepdims=True)
    byte = np.maximum(np.where(amax > 0, np.frexp(amax)[1] - 1 + 127, 0) - down, 1)
    scale = np.exp2(byte - 127.0)
    codes = (blocks / scale).astype(np.float32).astype(dtype).astype(np.float64)
    return np.moveaxis((codes * scale).reshape(v.shape), -1, axis)


WIDE = False


def mx_kscale(k):
    if not WIDE:
        return np.ones(k)
    levels = np.array([10, -10, 5, -5, 0])
    a = np.random.permutation(np.resize(levels, k // 512 * 4)).reshape(k // 512, 4)
    idx = np.arange(k)
    return np.exp2(a[idx // 512, idx % 128 // 32])


BF16 = ml_dtypes.bfloat16


def bf(x):
    return np.asarray(x, np.float32).astype(BF16)


def f64(x):
    return np.asarray(x).astype(np.float64)


E2M1 = np.array([0.0, 0.5, 1.0, 1.5, 2.0, 3.0, 4.0, 6.0, -0.0, -0.5, -1.0, -1.5, -2.0, -3.0, -4.0, -6.0])


def pack_weight(w, fmt):
    k, n = w.shape
    w = f64(bf(w)).reshape(k // 32, 32, n)
    amax = np.abs(w).max(1)
    if fmt == "e4m3":
        byte = np.frexp(amax)[1] - 1 + 127 - 7
    else:
        mant, ex = np.frexp(amax / 6.0)
        byte = np.where(mant > 0.5, ex, ex - 1) + 127
    byte = np.clip(np.where(amax > 0, byte, 1), 1, 254)
    scaled = (w * np.exp2(127.0 - byte)[:, None, :]).reshape(k, n).astype(np.float32)
    by_word = np.ascontiguousarray(scaled.reshape(k // 512, 128, 4, n).transpose(0, 1, 3, 2))
    if fmt == "e4m3":
        words = by_word.astype(ml_dtypes.float8_e4m3fn).view(np.uint8)
    else:
        c = by_word.astype(ml_dtypes.float4_e2m1fn).view(np.uint8) & 0xF
        words = c[..., 0::2] | (c[..., 1::2] << 4)
    return np.ascontiguousarray(words), np.ascontiguousarray(byte.astype(np.uint8).reshape(k // 512, 16, n))


def unpack_weight(words, scales, fmt):
    g, p, n, _ = words.shape
    if fmt == "e4m3":
        vals = np.ascontiguousarray(words).view(ml_dtypes.float8_e4m3fn).astype(np.float64)
    else:
        nib = np.empty((g, p, n, 4), np.uint8)
        nib[..., 0::2] = words & 0xF
        nib[..., 1::2] = words >> 4
        vals = E2M1[nib]
    vals = vals * np.repeat(np.exp2(scales.astype(np.float64) - 127.0), 8, axis=1)[..., None]
    return vals.transpose(0, 1, 3, 2).reshape(g * 512, n)

def pack4(w):
    words, scales = pack_weight(w, "e2m1")
    return words.reshape(words.shape[0], 128, -1), scales


def unpack4(words, scales):
    return unpack_weight(words.reshape(words.shape[0], 128, -1, 2), scales, "e2m1")


B, D0, D1, D2, D3 = 256, 1024, 1024, 1024, 1024
HEBB = 0.01
RATE = 0.001
BATCH_NUM = 1
C = HEBB * RATE / BATCH_NUM


def centred(s):
    return s / np.exp2(np.round(np.log2(s.mean())))


def setup_inputs():
    s = centred(mx_kscale(D2))
    vi = bf(np.maximum(3.0 + 5.0 * np.random.standard_normal((B, D2)), 0.0) * s)
    w = np.random.standard_normal((D3, D2)) * 0.9 / np.sqrt(D2) / s[None, :]
    words, scales = pack4(w.T)
    b = bf(3.0 + 1.5 * np.random.standard_normal(D3))
    return {"vi": vi, "W_words": words, "W_scales": scales, "b": b}


def reference(vi, W_words, W_scales, b):
    vi = f64(vi)
    vj = np.maximum((mxq(vi, 1, "e4m3") @ unpack4(W_words, W_scales)) + f64(b), 0.0)
    m = np.mean(vj, axis=0)
    out = vj + np.sum(vi, axis=1, keepdims=True) * (C * m)[None, :]
    return out, m

@@ -1,0 +1,165 @@
+from contextlib import ExitStack
+
+import concourse.mybir as mybir
+from concourse.masks import make_identity
+
+F32 = mybir.dt.float32
+BF16 = mybir.dt.bfloat16
+I32 = mybir.dt.int32
+U32 = mybir.dt.uint32
+U8 = mybir.dt.uint8
+FP8X4 = mybir.dt.float8_e4m3fn_x4
+FP4X4 = mybir.dt.float4_e2m1fn_x4
+ACT = mybir.ActivationFunctionType
+ALU = mybir.AluOpType
+
+P = 128
+PACK = 4
+K_PASS = P * PACK
+ROWS, K, OUTS = 256, 1024, 1024
+ROW_TILES = ROWS // P
+PASSES = K // K_PASS
+OUT_TILES = OUTS // P
+BANK_TILES = 4
+C = 0.01 * 0.001 / 1
+
+FLOPS = 2 * ROWS * K * OUTS
+
+
+def tile_optimalnet_pb_s_kernel(tc, vi, W_words, W_scales, b, out_0, out_1):
+    nc = tc.nc
+    with ExitStack() as ctx:
+        keep = ctx.enter_context(tc.tile_pool(name="keep", bufs=1))
+        work = ctx.enter_context(tc.tile_pool(name="work", bufs=3))
+        turned = ctx.enter_context(tc.psum_pool(name="turned", bufs=4))
+        sums = ctx.enter_context(tc.psum_pool(name="sums", bufs=3))
+        spread = ctx.enter_context(tc.psum_pool(name="spread", bufs=1))
+
+        vi_sb = keep.tile([P, ROW_TILES, K], BF16)
+        for rt in range(ROW_TILES):
+            nc.sync.dma_start(out=vi_sb[:, rt, :], in_=vi[rt * P : (rt + 1) * P, :])
+
+        w_scales = keep.tile([P, PASSES, OUTS], U8, align_bytes=64)
+        nc.vector.memset(w_scales[:].bitcast(I32), 0)
+        for r in range(4):
+            nc.sync.dma_start(
+                out=w_scales[r:P:32, :, :].bitcast(I32),
+                in_=W_scales.bitcast(I32)[:, r:16:4, :].rearrange("g q n -> q g n"),
+            )
+        w_words = keep.tile([P, PASSES, 2 * OUTS], U8, align_bytes=64)
+        nc.sync.dma_start(
+            out=w_words[:].bitcast(I32), in_=W_words.bitcast(I32).rearrange("g p n -> p g n")
+        )
+
+        b_rows = keep.tile([P, P], BF16)
+        nc.vector.memset(b_rows[:], 0.0)
+        nc.scalar.dma_start(out=b_rows[0:OUT_TILES, :], in_=b.rearrange("(j p) -> j p", p=P))
+
+        ident_f32 = keep.tile([P, P], F32)
+        make_identity(nc, ident_f32[:])
+        ident_bf16 = keep.tile([P, P], BF16)
+        make_identity(nc, ident_bf16[:])
+
+        b_turned = turned.tile([P, P], BF16, tag="turned")
+        nc.tensor.transpose(b_turned[:], b_rows[:], ident_bf16[:])
+        b_col = keep.tile([P, OUT_TILES], F32)
+        nc.vector.tensor_copy(out=b_col[:], in_=b_turned[:, 0:OUT_TILES])
+
+        grouped = keep.tile([P, ROW_TILES, PASSES, P * PACK], BF16, align_bytes=64)
+        vi_codes = keep.tile([P, ROW_TILES, PASSES * P], U32, align_bytes=64)
+        vi_scales = keep.tile([P, ROW_TILES, PASSES * P], U8, align_bytes=64)
+        row_term = keep.tile([P, ROW_TILES], F32)
+        for rt in range(ROW_TILES):
+            vi_pairs = vi_sb[:, rt, :].bitcast(F32)
+            for g in range(PASSES):
+                pairs_t = turned.tile([P, 2, P], F32, tag="turned")
+                for u in range(2):
+                    nc.tensor.transpose(
+                        pairs_t[:, u, :],
+                        vi_pairs[:, 256 * g + u : 256 * (g + 1) : 2],
+                        ident_f32[:],
+                    )
+                nc.vector.tensor_copy(
+                    out=grouped[:, rt, g, :].bitcast(F32).rearrange("p (r u) -> p r u", u=2),
+                    in_=pairs_t[:].rearrange("p u r -> p r u"),
+                )
+            nc.vector.quantize_mx(
+                out=vi_codes[:, rt, :].bitcast(FP8X4),
+                scales=vi_scales[:, rt, :],
+                in_=grouped[:, rt, :, :].rearrange("p g c -> p (g c)"),
+            )
+            scaled = work.tile([P, K], BF16)
+            nc.scalar.activation(
+                out=scaled[:],
+                in_=vi_sb[:, rt, :],
+                func=ACT.Copy,
+                scale=C / ROWS,
+                accum_out=row_term[:, rt : rt + 1],
+            )
+
+        row_term_all = spread.tile([P, ROWS], F32)
+        for rt in range(ROW_TILES):
+            nc.tensor.matmul(
+                out=row_term_all[:, rt * P : (rt + 1) * P],
+                lhsT=row_term[:, rt : rt + 1].to_broadcast([P, P]),
+                rhs=ident_f32[:],
+                start=True,
+                stop=True,
+            )
+
+        col_sum = keep.tile([P, P], F32)
+        nc.vector.memset(col_sum[:], 0.0)
+        for half in range(OUT_TILES // BANK_TILES):
+            corrected = work.tile([P, BANK_TILES, ROWS], F32)
+            for jj in range(BANK_TILES):
+                j = half * BANK_TILES + jj
+                acc = sums.tile([P, ROWS], F32)
+                for rt in range(ROW_TILES):
+                    for g in range(PASSES):
+                        nc.tensor.matmul_mx(
+                            out=acc[:, rt * P : (rt + 1) * P],
+                            lhsT=w_words[:, g, 2 * P * j : 2 * P * (j + 1)].bitcast(FP4X4),
+                            lhsT_scale=w_scales[:, g, P * j : P * (j + 1)],
+                            rhs=vi_codes[:, rt, P * g : P * (g + 1)].bitcast(FP8X4),
+                            rhs_scale=vi_scales[:, rt, P * g : P * (g + 1)],
+                            start=(g == 0),
+                            stop=(g == PASSES - 1),
+                        )
+                vj = work.tile([P, ROWS], F32)
+                nc.scalar.activation(
+                    out=vj[:],
+                    in_=acc[:],
+                    func=ACT.Relu,
+                    bias=b_col[:, j : j + 1],
+                    scale=1.0,
+                    accum_out=col_sum[:, j : j + 1],
+                )
+                nc.vector.scalar_tensor_tensor(
+                    out=corrected[:, jj, :],
+                    in0=row_term_all[:],
+                    scalar=col_sum[:, j : j + 1],
+                    in1=vj[:],
+                    op0=ALU.mult,
+                    op1=ALU.add,
+                )
+            for rt in range(ROW_TILES):
+                back = turned.tile([P, BANK_TILES * P], F32, tag="turned")
+                for jj in range(BANK_TILES):
+                    nc.tensor.transpose(
+                        back[:, jj * P : (jj + 1) * P],
+                        corrected[:, jj, rt * P : (rt + 1) * P],
+                        ident_f32[:],
+                    )
+                out_sb = work.tile([P, BANK_TILES * P], F32)
+                if rt == 0:
+                    nc.scalar.copy(out=out_sb[:], in_=back[:])
+                else:
+                    nc.vector.tensor_copy(out=out_sb[:], in_=back[:])
+                cols = slice(half * BANK_TILES * P, (half + 1) * BANK_TILES * P)
+                nc.sync.dma_start(out=out_0[rt * P : (rt + 1) * P, cols], in_=out_sb[:])
+
+        m_turned = turned.tile([P, P], F32, tag="turned")
+        nc.tensor.transpose(m_turned[:], col_sum[:], ident_f32[:])
+        m_rows = keep.tile([OUT_TILES, P], F32)
+        nc.scalar.mul(m_rows[:], m_turned[0:OUT_TILES, :], 1.0 / ROWS)
+        nc.sync.dma_start(out=out_1.rearrange("(j p) -> j p", p=P), in_=m_rows[:])

@@ -20,7 +20,10 @@ ROWS, K, OUTS = 256, 1024, 1024
 ROW_TILES = ROWS // P
 PASSES = K // K_PASS
 OUT_TILES = OUTS // P
-BANK_TILES = 4
+GROUP = 2
+STEPS = OUT_TILES // GROUP
+TURN_LAG = 2
+LEAVE_LAG = 3
 C = 0.01 * 0.001 / 1
 
 FLOPS = 2 * ROWS * K * OUTS
@@ -30,10 +33,11 @@ def tile_optimalnet_pb_s_kernel(tc, vi, W_words, W_scales, b, out_0, out_1):
     nc = tc.nc
     with ExitStack() as ctx:
         keep = ctx.enter_context(tc.tile_pool(name="keep", bufs=1))
-        work = ctx.enter_context(tc.tile_pool(name="work", bufs=3))
+        work = ctx.enter_context(tc.tile_pool(name="work", bufs=4))
         turned = ctx.enter_context(tc.psum_pool(name="turned", bufs=4))
         sums = ctx.enter_context(tc.psum_pool(name="sums", bufs=3))
         spread = ctx.enter_context(tc.psum_pool(name="spread", bufs=1))
+        ctx.enter_context(tc.manual_schedule())
 
         vi_sb = keep.tile([P, ROW_TILES, K], BF16)
         for rt in range(ROW_TILES):
@@ -54,11 +58,13 @@ def tile_optimalnet_pb_s_kernel(tc, vi, W_words, W_scales, b, out_0, out_1):
         b_rows = keep.tile([P, P], BF16)
         nc.vector.memset(b_rows[:], 0.0)
         nc.scalar.dma_start(out=b_rows[0:OUT_TILES, :], in_=b.rearrange("(j p) -> j p", p=P))
+        col_sum = keep.tile([P, P], F32)
+        nc.vector.memset(col_sum[:], 0.0)
 
-        ident_f32 = keep.tile([P, P], F32)
-        make_identity(nc, ident_f32[:])
         ident_bf16 = keep.tile([P, P], BF16)
         make_identity(nc, ident_bf16[:])
+        ident_f32 = keep.tile([P, P], F32)
+        make_identity(nc, ident_f32[:])
 
         b_turned = turned.tile([P, P], BF16, tag="turned")
         nc.tensor.transpose(b_turned[:], b_rows[:], ident_bf16[:])
@@ -98,68 +104,96 @@ def tile_optimalnet_pb_s_kernel(tc, vi, W_words, W_scales, b, out_0, out_1):
             )
 
         row_term_all = spread.tile([P, ROWS], F32)
-        for rt in range(ROW_TILES):
-            nc.tensor.matmul(
-                out=row_term_all[:, rt * P : (rt + 1) * P],
-                lhsT=row_term[:, rt : rt + 1].to_broadcast([P, P]),
-                rhs=ident_f32[:],
-                start=True,
-                stop=True,
+
+        def spread_row_term():
+            for rt in range(ROW_TILES):
+                nc.tensor.matmul(
+                    out=row_term_all[:, rt * P : (rt + 1) * P],
+                    lhsT=row_term[:, rt : rt + 1].to_broadcast([P, P]),
+                    rhs=ident_f32[:],
+                    start=True,
+                    stop=True,
+                )
+
+        acc_of = {}
+        back_of = {}
+        corrected = keep.tile([P, OUT_TILES, ROWS], F32)
+
+        def multiply(j):
+            acc = sums.tile([P, ROWS], F32)
+            acc_of[j] = acc
+            for rt in range(ROW_TILES):
+                for g in range(PASSES):
+                    nc.tensor.matmul_mx(
+                        out=acc[:, rt * P : (rt + 1) * P],
+                        lhsT=w_words[:, g, 2 * P * j : 2 * P * (j + 1)].bitcast(FP4X4),
+                        lhsT_scale=w_scales[:, g, P * j : P * (j + 1)],
+                        rhs=vi_codes[:, rt, P * g : P * (g + 1)].bitcast(FP8X4),
+                        rhs_scale=vi_scales[:, rt, P * g : P * (g + 1)],
+                        start=(g == 0),
+                        stop=(g == PASSES - 1),
+                    )
+
+        def finish(j):
+            vj = work.tile([P, ROWS], F32)
+            nc.scalar.activation(
+                out=vj[:],
+                in_=acc_of[j][:],
+                func=ACT.Relu,
+                bias=b_col[:, j : j + 1],
+                scale=1.0,
+                accum_out=col_sum[:, j : j + 1],
+            )
+            nc.vector.scalar_tensor_tensor(
+                out=corrected[:, j, :],
+                in0=row_term_all[:],
+                scalar=col_sum[:, j : j + 1],
+                in1=vj[:],
+                op0=ALU.mult,
+                op1=ALU.add,
             )
 
-        col_sum = keep.tile([P, P], F32)
-        nc.vector.memset(col_sum[:], 0.0)
-        for half in range(OUT_TILES // BANK_TILES):
-            corrected = work.tile([P, BANK_TILES, ROWS], F32)
-            for jj in range(BANK_TILES):
-                j = half * BANK_TILES + jj
-                acc = sums.tile([P, ROWS], F32)
-                for rt in range(ROW_TILES):
-                    for g in range(PASSES):
-                        nc.tensor.matmul_mx(
-                            out=acc[:, rt * P : (rt + 1) * P],
-                            lhsT=w_words[:, g, 2 * P * j : 2 * P * (j + 1)].bitcast(FP4X4),
-                            lhsT_scale=w_scales[:, g, P * j : P * (j + 1)],
-                            rhs=vi_codes[:, rt, P * g : P * (g + 1)].bitcast(FP8X4),
-                            rhs_scale=vi_scales[:, rt, P * g : P * (g + 1)],
-                            start=(g == 0),
-                            stop=(g == PASSES - 1),
-                        )
-                vj = work.tile([P, ROWS], F32)
-                nc.scalar.activation(
-                    out=vj[:],
-                    in_=acc[:],
-                    func=ACT.Relu,
-                    bias=b_col[:, j : j + 1],
-                    scale=1.0,
-                    accum_out=col_sum[:, j : j + 1],
-                )
-                nc.vector.scalar_tensor_tensor(
-                    out=corrected[:, jj, :],
-                    in0=row_term_all[:],
-                    scalar=col_sum[:, j : j + 1],
-                    in1=vj[:],
-                    op0=ALU.mult,
-                    op1=ALU.add,
-                )
+        def turn_back(s):
             for rt in range(ROW_TILES):
-                back = turned.tile([P, BANK_TILES * P], F32, tag="turned")
-                for jj in range(BANK_TILES):
+                back = turned.tile([P, GROUP * P], F32, tag="turned")
+                back_of[(s, rt)] = back
+            for i in range(GROUP):
+                for rt in range(ROW_TILES):
                     nc.tensor.transpose(
-                        back[:, jj * P : (jj + 1) * P],
-                        corrected[:, jj, rt * P : (rt + 1) * P],
+                        back_of[(s, rt)][:, i * P : (i + 1) * P],
+                        corrected[:, s * GROUP + i, rt * P : (rt + 1) * P],
                         ident_f32[:],
                     )
-                out_sb = work.tile([P, BANK_TILES * P], F32)
+
+        def leave(s):
+            for rt in range(ROW_TILES):
+                out_sb = work.tile([P, GROUP * P], F32)
                 if rt == 0:
-                    nc.scalar.copy(out=out_sb[:], in_=back[:])
+                    nc.scalar.copy(out=out_sb[:], in_=back_of[(s, rt)][:])
                 else:
-                    nc.vector.tensor_copy(out=out_sb[:], in_=back[:])
-                cols = slice(half * BANK_TILES * P, (half + 1) * BANK_TILES * P)
+                    nc.vector.tensor_copy(out=out_sb[:], in_=back_of[(s, rt)][:])
+                cols = slice(s * GROUP * P, (s + 1) * GROUP * P)
                 nc.sync.dma_start(out=out_0[rt * P : (rt + 1) * P, cols], in_=out_sb[:])
 
-        m_turned = turned.tile([P, P], F32, tag="turned")
-        nc.tensor.transpose(m_turned[:], col_sum[:], ident_f32[:])
-        m_rows = keep.tile([OUT_TILES, P], F32)
-        nc.scalar.mul(m_rows[:], m_turned[0:OUT_TILES, :], 1.0 / ROWS)
-        nc.sync.dma_start(out=out_1.rearrange("(j p) -> j p", p=P), in_=m_rows[:])
+        def mean_out():
+            m_turned = turned.tile([P, P], F32, tag="turned")
+            nc.tensor.transpose(m_turned[:], col_sum[:], ident_f32[:])
+            m_rows = keep.tile([OUT_TILES, P], F32)
+            nc.scalar.mul(m_rows[:], m_turned[0:OUT_TILES, :], 1.0 / ROWS)
+            nc.sync.dma_start(out=out_1.rearrange("(j p) -> j p", p=P), in_=m_rows[:])
+
+        for step in range(STEPS + LEAVE_LAG):
+            if step >= LEAVE_LAG:
+                leave(step - LEAVE_LAG)
+            if step < STEPS:
+                tiles = range(step * GROUP, (step + 1) * GROUP)
+                for j in tiles:
+                    multiply(j)
+                if step == 0:
+                    spread_row_term()
+                for j in tiles:
+                    finish(j)
+            if step == STEPS:
+                mean_out()
+            if TURN_LAG <= step < STEPS + TURN_LAG:
+                turn_back(step - TURN_LAG)

@@ -20,10 +20,8 @@ ROWS, K, OUTS = 256, 1024, 1024
 ROW_TILES = ROWS // P
 PASSES = K // K_PASS
 OUT_TILES = OUTS // P
-GROUP = 2
-STEPS = OUT_TILES // GROUP
-TURN_LAG = 2
-LEAVE_LAG = 3
+BANK_TILES = 4
+HALVES = OUT_TILES // BANK_TILES
 C = 0.01 * 0.001 / 1
 
 FLOPS = 2 * ROWS * K * OUTS
@@ -39,6 +37,10 @@ def tile_optimalnet_pb_s_kernel(tc, vi, W_words, W_scales, b, out_0, out_1):
         spread = ctx.enter_context(tc.psum_pool(name="spread", bufs=1))
         ctx.enter_context(tc.manual_schedule())
 
+        b_rows = keep.tile([P, P], BF16)
+        nc.vector.memset(b_rows[:], 0.0)
+        nc.scalar.dma_start(out=b_rows[0:OUT_TILES, :], in_=b.rearrange("(j p) -> j p", p=P))
+
         vi_sb = keep.tile([P, ROW_TILES, K], BF16)
         for rt in range(ROW_TILES):
             nc.sync.dma_start(out=vi_sb[:, rt, :], in_=vi[rt * P : (rt + 1) * P, :])
@@ -51,31 +53,33 @@ def tile_optimalnet_pb_s_kernel(tc, vi, W_words, W_scales, b, out_0, out_1):
                 in_=W_scales.bitcast(I32)[:, r:16:4, :].rearrange("g q n -> q g n"),
             )
         w_words = keep.tile([P, PASSES, 2 * OUTS], U8, align_bytes=64)
-        nc.sync.dma_start(
-            out=w_words[:].bitcast(I32), in_=W_words.bitcast(I32).rearrange("g p n -> p g n")
-        )
+        for h in range(HALVES):
+            word_bytes = slice(h * 2 * OUTS // HALVES, (h + 1) * 2 * OUTS // HALVES)
+            nc.sync.dma_start(
+                out=w_words[:, :, word_bytes].bitcast(I32),
+                in_=W_words[:, :, word_bytes].bitcast(I32).rearrange("g p n -> p g n"),
+            )
 
-        b_rows = keep.tile([P, P], BF16)
-        nc.vector.memset(b_rows[:], 0.0)
-        nc.scalar.dma_start(out=b_rows[0:OUT_TILES, :], in_=b.rearrange("(j p) -> j p", p=P))
         col_sum = keep.tile([P, P], F32)
         nc.vector.memset(col_sum[:], 0.0)
-
-        ident_bf16 = keep.tile([P, P], BF16)
-        make_identity(nc, ident_bf16[:])
         ident_f32 = keep.tile([P, P], F32)
         make_identity(nc, ident_f32[:])
-
-        b_turned = turned.tile([P, P], BF16, tag="turned")
-        nc.tensor.transpose(b_turned[:], b_rows[:], ident_bf16[:])
-        b_col = keep.tile([P, OUT_TILES], F32)
-        nc.vector.tensor_copy(out=b_col[:], in_=b_turned[:, 0:OUT_TILES])
+        ident_bf16 = keep.tile([P, P], BF16)
+        make_identity(nc, ident_bf16[:])
 
         grouped = keep.tile([P, ROW_TILES, PASSES, P * PACK], BF16, align_bytes=64)
         vi_codes = keep.tile([P, ROW_TILES, PASSES * P], U32, align_bytes=64)
         vi_scales = keep.tile([P, ROW_TILES, PASSES * P], U8, align_bytes=64)
         row_term = keep.tile([P, ROW_TILES], F32)
         for rt in range(ROW_TILES):
+            scaled = work.tile([P, K], BF16)
+            nc.scalar.activation(
+                out=scaled[:],
+                in_=vi_sb[:, rt, :],
+                func=ACT.Copy,
+                scale=C / ROWS,
+                accum_out=row_term[:, rt : rt + 1],
+            )
             vi_pairs = vi_sb[:, rt, :].bitcast(F32)
             for g in range(PASSES):
                 pairs_t = turned.tile([P, 2, P], F32, tag="turned")
@@ -94,34 +98,23 @@ def tile_optimalnet_pb_s_kernel(tc, vi, W_words, W_scales, b, out_0, out_1):
                 scales=vi_scales[:, rt, :],
                 in_=grouped[:, rt, :, :].rearrange("p g c -> p (g c)"),
             )
-            scaled = work.tile([P, K], BF16)
-            nc.scalar.activation(
-                out=scaled[:],
-                in_=vi_sb[:, rt, :],
-                func=ACT.Copy,
-                scale=C / ROWS,
-                accum_out=row_term[:, rt : rt + 1],
-            )
+
+        b_turned = turned.tile([P, P], BF16, tag="turned")
+        nc.tensor.transpose(b_turned[:], b_rows[:], ident_bf16[:])
+        b_col = keep.tile([P, OUT_TILES], F32)
+        nc.vector.tensor_copy(out=b_col[:], in_=b_turned[:, 0:OUT_TILES])
 
         row_term_all = spread.tile([P, ROWS], F32)
+        for rt in range(ROW_TILES):
+            nc.tensor.transpose(
+                row_term_all[:, rt * P : (rt + 1) * P],
+                row_term[:, rt : rt + 1].to_broadcast([P, P]),
+                ident_f32[:],
+            )
 
-        def spread_row_term():
-            for rt in range(ROW_TILES):
-                nc.tensor.matmul(
-                    out=row_term_all[:, rt * P : (rt + 1) * P],
-                    lhsT=row_term[:, rt : rt + 1].to_broadcast([P, P]),
-                    rhs=ident_f32[:],
-                    start=True,
-                    stop=True,
-                )
-
-        acc_of = {}
-        back_of = {}
         corrected = keep.tile([P, OUT_TILES, ROWS], F32)
-
-        def multiply(j):
-            acc = sums.tile([P, ROWS], F32)
-            acc_of[j] = acc
+        for j in range(OUT_TILES):
+            acc = sums.tile([P, ROWS], F32, tag="acc")
             for rt in range(ROW_TILES):
                 for g in range(PASSES):
                     nc.tensor.matmul_mx(
@@ -133,12 +126,10 @@ def tile_optimalnet_pb_s_kernel(tc, vi, W_words, W_scales, b, out_0, out_1):
                         start=(g == 0),
                         stop=(g == PASSES - 1),
                     )
-
-        def finish(j):
             vj = work.tile([P, ROWS], F32)
             nc.scalar.activation(
                 out=vj[:],
-                in_=acc_of[j][:],
+                in_=acc[:],
                 func=ACT.Relu,
                 bias=b_col[:, j : j + 1],
                 scale=1.0,
@@ -153,47 +144,32 @@ def tile_optimalnet_pb_s_kernel(tc, vi, W_words, W_scales, b, out_0, out_1):
                 op1=ALU.add,
             )
 
-        def turn_back(s):
+        back_of = {}
+        for h in range(HALVES):
             for rt in range(ROW_TILES):
-                back = turned.tile([P, GROUP * P], F32, tag="turned")
-                back_of[(s, rt)] = back
-            for i in range(GROUP):
-                for rt in range(ROW_TILES):
-                    nc.tensor.transpose(
-                        back_of[(s, rt)][:, i * P : (i + 1) * P],
-                        corrected[:, s * GROUP + i, rt * P : (rt + 1) * P],
-                        ident_f32[:],
-                    )
+                back = turned.tile([P, BANK_TILES * P], F32, tag="turned")
+                back_of[(h, rt)] = back
+        m_turned = sums.tile([P, P], F32, tag="acc")
+        for j in range(OUT_TILES):
+            if j == OUT_TILES - 1:
+                nc.tensor.transpose(m_turned[:], col_sum[:], ident_f32[:])
+            for rt in range(ROW_TILES):
+                nc.tensor.transpose(
+                    back_of[(j // BANK_TILES, rt)][:, (j % BANK_TILES) * P : (j % BANK_TILES + 1) * P],
+                    corrected[:, j, rt * P : (rt + 1) * P],
+                    ident_f32[:],
+                )
 
-        def leave(s):
+        for h in range(HALVES):
             for rt in range(ROW_TILES):
-                out_sb = work.tile([P, GROUP * P], F32)
+                out_sb = work.tile([P, BANK_TILES * P], F32)
                 if rt == 0:
-                    nc.scalar.copy(out=out_sb[:], in_=back_of[(s, rt)][:])
+                    nc.scalar.copy(out=out_sb[:], in_=back_of[(h, rt)][:])
                 else:
-                    nc.vector.tensor_copy(out=out_sb[:], in_=back_of[(s, rt)][:])
-                cols = slice(s * GROUP * P, (s + 1) * GROUP * P)
+                    nc.vector.tensor_copy(out=out_sb[:], in_=back_of[(h, rt)][:])
+                cols = slice(h * BANK_TILES * P, (h + 1) * BANK_TILES * P)
                 nc.sync.dma_start(out=out_0[rt * P : (rt + 1) * P, cols], in_=out_sb[:])
-
-        def mean_out():
-            m_turned = turned.tile([P, P], F32, tag="turned")
-            nc.tensor.transpose(m_turned[:], col_sum[:], ident_f32[:])
-            m_rows = keep.tile([OUT_TILES, P], F32)
-            nc.scalar.mul(m_rows[:], m_turned[0:OUT_TILES, :], 1.0 / ROWS)
-            nc.sync.dma_start(out=out_1.rearrange("(j p) -> j p", p=P), in_=m_rows[:])
-
-        for step in range(STEPS + LEAVE_LAG):
-            if step >= LEAVE_LAG:
-                leave(step - LEAVE_LAG)
-            if step < STEPS:
-                tiles = range(step * GROUP, (step + 1) * GROUP)
-                for j in tiles:
-                    multiply(j)
-                if step == 0:
-                    spread_row_term()
-                for j in tiles:
-                    finish(j)
-            if step == STEPS:
-                mean_out()
-            if TURN_LAG <= step < STEPS + TURN_LAG:
-                turn_back(step - TURN_LAG)
+            if h == 0:
+                m_rows = keep.tile([OUT_TILES, P], F32)
+                nc.scalar.mul(m_rows[:], m_turned[0:OUT_TILES, :], 1.0 / ROWS)
+                nc.sync.dma_start(out=out_1.rearrange("(j p) -> j p", p=P), in_=m_rows[:])

@@ -21,6 +21,7 @@ ROW_TILES = ROWS // P
 PASSES = K // K_PASS
 OUT_TILES = OUTS // P
 BANK_TILES = 4
+SUM_BANKS = 3
 HALVES = OUT_TILES // BANK_TILES
 C = 0.01 * 0.001 / 1
 
@@ -33,7 +34,7 @@ def tile_optimalnet_pb_s_kernel(tc, vi, W_words, W_scales, b, out_0, out_1):
         keep = ctx.enter_context(tc.tile_pool(name="keep", bufs=1))
         work = ctx.enter_context(tc.tile_pool(name="work", bufs=4))
         turned = ctx.enter_context(tc.psum_pool(name="turned", bufs=4))
-        sums = ctx.enter_context(tc.psum_pool(name="sums", bufs=3))
+        sums = ctx.enter_context(tc.psum_pool(name="sums", bufs=SUM_BANKS))
         spread = ctx.enter_context(tc.psum_pool(name="spread", bufs=1))
         ctx.enter_context(tc.manual_schedule())
 
@@ -104,6 +105,27 @@ def tile_optimalnet_pb_s_kernel(tc, vi, W_words, W_scales, b, out_0, out_1):
         b_col = keep.tile([P, OUT_TILES], F32)
         nc.vector.tensor_copy(out=b_col[:], in_=b_turned[:, 0:OUT_TILES])
 
+        acc_of = {}
+
+        def multiply(j, rt):
+            for g in range(PASSES):
+                nc.tensor.matmul_mx(
+                    out=acc_of[j][:, rt * P : (rt + 1) * P],
+                    lhsT=w_words[:, g, 2 * P * j : 2 * P * (j + 1)].bitcast(FP4X4),
+                    lhsT_scale=w_scales[:, g, P * j : P * (j + 1)],
+                    rhs=vi_codes[:, rt, P * g : P * (g + 1)].bitcast(FP8X4),
+                    rhs_scale=vi_scales[:, rt, P * g : P * (g + 1)],
+                    start=(g == 0),
+                    stop=(g == PASSES - 1),
+                )
+
+        for rt in range(ROW_TILES):
+            for j in range(SUM_BANKS):
+                if rt == 0:
+                    acc = sums.tile([P, ROWS], F32, tag="acc")
+                    acc_of[j] = acc
+                multiply(j, rt)
+
         row_term_all = spread.tile([P, ROWS], F32)
         for rt in range(ROW_TILES):
             nc.tensor.transpose(
@@ -114,22 +136,15 @@ def tile_optimalnet_pb_s_kernel(tc, vi, W_words, W_scales, b, out_0, out_1):
 
         corrected = keep.tile([P, OUT_TILES, ROWS], F32)
         for j in range(OUT_TILES):
-            acc = sums.tile([P, ROWS], F32, tag="acc")
-            for rt in range(ROW_TILES):
-                for g in range(PASSES):
-                    nc.tensor.matmul_mx(
-                        out=acc[:, rt * P : (rt + 1) * P],
-                        lhsT=w_words[:, g, 2 * P * j : 2 * P * (j + 1)].bitcast(FP4X4),
-                        lhsT_scale=w_scales[:, g, P * j : P * (j + 1)],
-                        rhs=vi_codes[:, rt, P * g : P * (g + 1)].bitcast(FP8X4),
-                        rhs_scale=vi_scales[:, rt, P * g : P * (g + 1)],
-                        start=(g == 0),
-                        stop=(g == PASSES - 1),
-                    )
+            if j >= SUM_BANKS:
+                acc = sums.tile([P, ROWS], F32, tag="acc")
+                acc_of[j] = acc
+                for rt in range(ROW_TILES):
+                    multiply(j, rt)
             vj = work.tile([P, ROWS], F32)
             nc.scalar.activation(
                 out=vj[:],
-                in_=acc[:],
+                in_=acc_of[j][:],
                 func=ACT.Relu,
                 bias=b_col[:, j : j + 1],
                 scale=1.0,

@@ -38,13 +38,9 @@ def tile_optimalnet_pb_s_kernel(tc, vi, W_words, W_scales, b, out_0, out_1):
         spread = ctx.enter_context(tc.psum_pool(name="spread", bufs=1))
         ctx.enter_context(tc.manual_schedule())
 
-        b_rows = keep.tile([P, P], BF16)
-        nc.vector.memset(b_rows[:], 0.0)
-        nc.scalar.dma_start(out=b_rows[0:OUT_TILES, :], in_=b.rearrange("(j p) -> j p", p=P))
-
         vi_sb = keep.tile([P, ROW_TILES, K], BF16)
         for rt in range(ROW_TILES):
-            nc.sync.dma_start(out=vi_sb[:, rt, :], in_=vi[rt * P : (rt + 1) * P, :])
+            nc.scalar.dma_start(out=vi_sb[:, rt, :], in_=vi[rt * P : (rt + 1) * P, :])
 
         w_scales = keep.tile([P, PASSES, OUTS], U8, align_bytes=64)
         nc.vector.memset(w_scales[:].bitcast(I32), 0)
@@ -53,6 +49,9 @@ def tile_optimalnet_pb_s_kernel(tc, vi, W_words, W_scales, b, out_0, out_1):
                 out=w_scales[r:P:32, :, :].bitcast(I32),
                 in_=W_scales.bitcast(I32)[:, r:16:4, :].rearrange("g q n -> q g n"),
             )
+        b_rows = keep.tile([P, P], BF16)
+        nc.vector.memset(b_rows[:], 0.0)
+        nc.sync.dma_start(out=b_rows[0:OUT_TILES, :], in_=b.rearrange("(j p) -> j p", p=P))
         w_words = keep.tile([P, PASSES, 2 * OUTS], U8, align_bytes=64)
         for h in range(HALVES):
             word_bytes = slice(h * 2 * OUTS // HALVES, (h + 1) * 2 * OUTS // HALVES)

@@ -38,6 +38,18 @@ def tile_optimalnet_pb_s_kernel(tc, vi, W_words, W_scales, b, out_0, out_1):
         spread = ctx.enter_context(tc.psum_pool(name="spread", bufs=1))
         ctx.enter_context(tc.manual_schedule())
 
+        warm_in = keep.tile([P, P], F32)
+        nc.gpsimd.memset(warm_in[:], 0.0)
+        spread_bank = spread.tile([P, 4 * P], F32)
+        row_term_all = spread_bank[:, 0:ROWS]
+        warm_out = spread_bank[:, ROWS : ROWS + P]
+
+        def warm(passes):
+            for i in range(passes):
+                nc.tensor.matmul(warm_out, lhsT=warm_in[:], rhs=warm_in[:], start=True, stop=True)
+
+        warm(3)
+
         vi_sb = keep.tile([P, ROW_TILES, K], BF16)
         for rt in range(ROW_TILES):
             nc.scalar.dma_start(out=vi_sb[:, rt, :], in_=vi[rt * P : (rt + 1) * P, :])
@@ -93,6 +105,8 @@ def tile_optimalnet_pb_s_kernel(tc, vi, W_words, W_scales, b, out_0, out_1):
                     out=grouped[:, rt, g, :].bitcast(F32).rearrange("p (r u) -> p r u", u=2),
                     in_=pairs_t[:].rearrange("p u r -> p r u"),
                 )
+            if rt == 0:
+                warm(1)
             nc.vector.quantize_mx(
                 out=vi_codes[:, rt, :].bitcast(FP8X4),
                 scales=vi_scales[:, rt, :],
@@ -101,6 +115,7 @@ def tile_optimalnet_pb_s_kernel(tc, vi, W_words, W_scales, b, out_0, out_1):
 
         b_turned = turned.tile([P, P], BF16, tag="turned")
         nc.tensor.transpose(b_turned[:], b_rows[:], ident_bf16[:])
+        warm(3)
         b_col = keep.tile([P, OUT_TILES], F32)
         nc.vector.tensor_copy(out=b_col[:], in_=b_turned[:, 0:OUT_TILES])
 
@@ -125,7 +140,6 @@ def tile_optimalnet_pb_s_kernel(tc, vi, W_words, W_scales, b, out_0, out_1):
                     acc_of[j] = acc
                 multiply(j, rt)
 
-        row_term_all = spread.tile([P, ROWS], F32)
         for rt in range(ROW_TILES):
             nc.tensor.transpose(
                 row_term_all[:, rt * P : (rt + 1) * P],
@@ -151,7 +165,7 @@ def tile_optimalnet_pb_s_kernel(tc, vi, W_words, W_scales, b, out_0, out_1):
             )
             nc.vector.scalar_tensor_tensor(
                 out=corrected[:, j, :],
-                in0=row_term_all[:],
+                in0=row_term_all,
                 scalar=col_sum[:, j : j + 1],
                 in1=vj[:],
                 op0=ALU.mult,

@@ -21,9 +21,10 @@ ROW_TILES = ROWS // P
 PASSES = K // K_PASS
 OUT_TILES = OUTS // P
 BANK_TILES = 4
-SUM_BANKS = 3
+SUM_BANKS = 4
 HALVES = OUT_TILES // BANK_TILES
 C = 0.01 * 0.001 / 1
+EARLY_TILES = 2
 
 FLOPS = 2 * ROWS * K * OUTS
 
@@ -33,7 +34,7 @@ def tile_optimalnet_pb_s_kernel(tc, vi, W_words, W_scales, b, out_0, out_1):
     with ExitStack() as ctx:
         keep = ctx.enter_context(tc.tile_pool(name="keep", bufs=1))
         work = ctx.enter_context(tc.tile_pool(name="work", bufs=4))
-        turned = ctx.enter_context(tc.psum_pool(name="turned", bufs=4))
+        turned = ctx.enter_context(tc.psum_pool(name="turned", bufs=3))
         sums = ctx.enter_context(tc.psum_pool(name="sums", bufs=SUM_BANKS))
         spread = ctx.enter_context(tc.psum_pool(name="spread", bufs=1))
         ctx.enter_context(tc.manual_schedule())
@@ -83,30 +84,53 @@ def tile_optimalnet_pb_s_kernel(tc, vi, W_words, W_scales, b, out_0, out_1):
         vi_codes = keep.tile([P, ROW_TILES, PASSES * P], U32, align_bytes=64)
         vi_scales = keep.tile([P, ROW_TILES, PASSES * P], U8, align_bytes=64)
         row_term = keep.tile([P, ROW_TILES], F32)
+
+        same = keep.tile([P, K], BF16)
+        row_sum = keep.tile([P, 1], F32)
+        nc.vector.tensor_scalar(
+            out=same[:],
+            in0=vi_sb[:, 0, :],
+            scalar1=1.0,
+            scalar2=None,
+            op0=ALU.mult,
+            op1=ALU.add,
+            accum_out=row_sum[:],
+        )
+        nc.vector.tensor_scalar(
+            out=row_term[:, 0:1], in0=row_sum[:], scalar1=C / ROWS, scalar2=None, op0=ALU.mult
+        )
+
+        pairs_of = {}
         for rt in range(ROW_TILES):
-            scaled = work.tile([P, K], BF16)
-            nc.scalar.activation(
-                out=scaled[:],
-                in_=vi_sb[:, rt, :],
-                func=ACT.Copy,
-                scale=C / ROWS,
-                accum_out=row_term[:, rt : rt + 1],
-            )
             vi_pairs = vi_sb[:, rt, :].bitcast(F32)
             for g in range(PASSES):
                 pairs_t = turned.tile([P, 2, P], F32, tag="turned")
+                pairs_of[(rt, g)] = pairs_t
                 for u in range(2):
                     nc.tensor.transpose(
                         pairs_t[:, u, :],
                         vi_pairs[:, 256 * g + u : 256 * (g + 1) : 2],
                         ident_f32[:],
                     )
-                nc.vector.tensor_copy(
-                    out=grouped[:, rt, g, :].bitcast(F32).rearrange("p (r u) -> p r u", u=2),
-                    in_=pairs_t[:].rearrange("p u r -> p r u"),
-                )
             if rt == 0:
-                warm(1)
+                warm(0)
+        for rt in range(ROW_TILES):
+            for g in range(PASSES):
+                dst = grouped[:, rt, g, :].bitcast(F32).rearrange("p (r u) -> p r u", u=2)
+                src = pairs_of[(rt, g)][:].rearrange("p u r -> p r u")
+                if g == 0:
+                    nc.vector.tensor_copy(out=dst, in_=src)
+                else:
+                    nc.scalar.copy(out=dst, in_=src)
+        scaled = keep.tile([P, K], BF16)
+        nc.scalar.activation(
+            out=scaled[:],
+            in_=vi_sb[:, 1, :],
+            func=ACT.Copy,
+            scale=C / ROWS,
+            accum_out=row_term[:, 1:2],
+        )
+        for rt in range(ROW_TILES):
             nc.vector.quantize_mx(
                 out=vi_codes[:, rt, :].bitcast(FP8X4),
                 scales=vi_scales[:, rt, :],
@@ -115,11 +139,15 @@ def tile_optimalnet_pb_s_kernel(tc, vi, W_words, W_scales, b, out_0, out_1):
 
         b_turned = turned.tile([P, P], BF16, tag="turned")
         nc.tensor.transpose(b_turned[:], b_rows[:], ident_bf16[:])
-        warm(3)
+        warm(1)
         b_col = keep.tile([P, OUT_TILES], F32)
         nc.vector.tensor_copy(out=b_col[:], in_=b_turned[:, 0:OUT_TILES])
 
         acc_of = {}
+
+        def open_sums(j):
+            acc = sums.tile([P, ROWS], F32, tag="acc")
+            acc_of[j] = acc
 
         def multiply(j, rt):
             for g in range(PASSES):
@@ -133,27 +161,24 @@ def tile_optimalnet_pb_s_kernel(tc, vi, W_words, W_scales, b, out_0, out_1):
                     stop=(g == PASSES - 1),
                 )
 
+        for j in range(SUM_BANKS):
+            open_sums(j)
         for rt in range(ROW_TILES):
-            for j in range(SUM_BANKS):
-                if rt == 0:
-                    acc = sums.tile([P, ROWS], F32, tag="acc")
-                    acc_of[j] = acc
+            for j in range(EARLY_TILES):
                 multiply(j, rt)
-
-        for rt in range(ROW_TILES):
-            nc.tensor.transpose(
-                row_term_all[:, rt * P : (rt + 1) * P],
-                row_term[:, rt : rt + 1].to_broadcast([P, P]),
-                ident_f32[:],
-            )
+        for j in range(EARLY_TILES, SUM_BANKS):
+            if j == 3:
+                for rt in range(ROW_TILES):
+                    nc.tensor.transpose(
+                        row_term_all[:, rt * P : (rt + 1) * P],
+                        row_term[:, rt : rt + 1].to_broadcast([P, P]),
+                        ident_f32[:],
+                    )
+            for rt in range(ROW_TILES):
+                multiply(j, rt)
 
         corrected = keep.tile([P, OUT_TILES, ROWS], F32)
         for j in range(OUT_TILES):
-            if j >= SUM_BANKS:
-                acc = sums.tile([P, ROWS], F32, tag="acc")
-                acc_of[j] = acc
-                for rt in range(ROW_TILES):
-                    multiply(j, rt)
             vj = work.tile([P, ROWS], F32)
             nc.scalar.activation(
                 out=vj[:],
@@ -171,11 +196,18 @@ def tile_optimalnet_pb_s_kernel(tc, vi, W_words, W_scales, b, out_0, out_1):
                 op0=ALU.mult,
                 op1=ALU.add,
             )
+            if j + SUM_BANKS < OUT_TILES:
+                open_sums(j + SUM_BANKS)
+                for rt in range(ROW_TILES):
+                    multiply(j + SUM_BANKS, rt)
 
         back_of = {}
         for h in range(HALVES):
             for rt in range(ROW_TILES):
-                back = turned.tile([P, BANK_TILES * P], F32, tag="turned")
+                if (h, rt) == (HALVES - 1, ROW_TILES - 1):
+                    back = sums.tile([P, BANK_TILES * P], F32, tag="acc")
+                else:
+                    back = turned.tile([P, BANK_TILES * P], F32, tag="turned")
                 back_of[(h, rt)] = back
         m_turned = sums.tile([P, P], F32, tag="acc")
         for j in range(OUT_TILES):

@@ -49,7 +49,7 @@ def tile_optimalnet_pb_s_kernel(tc, vi, W_words, W_scales, b, out_0, out_1):
             for i in range(passes):
                 nc.tensor.matmul(warm_out, lhsT=warm_in[:], rhs=warm_in[:], start=True, stop=True)
 
-        warm(3)
+        warm(4)
 
         vi_sb = keep.tile([P, ROW_TILES, K], BF16)
         for rt in range(ROW_TILES):
@@ -139,7 +139,7 @@ def tile_optimalnet_pb_s_kernel(tc, vi, W_words, W_scales, b, out_0, out_1):
 
         b_turned = turned.tile([P, P], BF16, tag="turned")
         nc.tensor.transpose(b_turned[:], b_rows[:], ident_bf16[:])
-        warm(1)
+        warm(2)
         b_col = keep.tile([P, OUT_TILES], F32)
         nc.vector.tensor_copy(out=b_col[:], in_=b_turned[:, 0:OUT_TILES])
 

@@ -39,16 +39,30 @@ def tile_optimalnet_pb_s_kernel(tc, vi, W_words, W_scales, b, out_0, out_1):
         spread = ctx.enter_context(tc.psum_pool(name="spread", bufs=1))
         ctx.enter_context(tc.manual_schedule())
 
-        warm_in = keep.tile([P, P], F32)
-        nc.gpsimd.memset(warm_in[:], 0.0)
+        zero = keep.tile([P, 2], F32)
+        nc.gpsimd.memset(zero[:], 0.0)
         spread_bank = spread.tile([P, 4 * P], F32)
         row_term_all = spread_bank[:, 0:ROWS]
         warm_out = spread_bank[:, ROWS : ROWS + P]
 
         def warm(passes):
             for i in range(passes):
-                nc.tensor.matmul(warm_out, lhsT=warm_in[:], rhs=warm_in[:], start=True, stop=True)
+                nc.tensor.matmul(
+                    warm_out,
+                    lhsT=zero[:, 0:1].to_broadcast([P, P]),
+                    rhs=zero[:, 0:1].to_broadcast([P, P]),
+                    start=True,
+                    stop=True,
+                )
 
+        zero_bf16 = zero[:].bitcast(BF16)
+        nc.tensor.matmul(
+            spread_bank[:],
+            lhsT=zero_bf16[:, 0:1].to_broadcast([P, P]),
+            rhs=zero_bf16[:, 0:1].to_broadcast([P, 4 * P]),
+            start=True,
+            stop=True,
+        )
         warm(4)
 
         vi_sb = keep.tile([P, ROW_TILES, K], BF16)

@@ -24,7 +24,7 @@ BANK_TILES = 4
 SUM_BANKS = 4
 HALVES = OUT_TILES // BANK_TILES
 C = 0.01 * 0.001 / 1
-EARLY_TILES = 2
+EARLY_TILES = 3
 
 FLOPS = 2 * ROWS * K * OUTS
 
@@ -132,7 +132,7 @@ def tile_optimalnet_pb_s_kernel(tc, vi, W_words, W_scales, b, out_0, out_1):
             for g in range(PASSES):
                 dst = grouped[:, rt, g, :].bitcast(F32).rearrange("p (r u) -> p r u", u=2)
                 src = pairs_of[(rt, g)][:].rearrange("p u r -> p r u")
-                if g == 0:
+                if (rt, g) == (0, 0):
                     nc.vector.tensor_copy(out=dst, in_=src)
                 else:
                     nc.scalar.copy(out=dst, in_=src)
@@ -177,19 +177,17 @@ def tile_optimalnet_pb_s_kernel(tc, vi, W_words, W_scales, b, out_0, out_1):
 
         for j in range(SUM_BANKS):
             open_sums(j)
-        for rt in range(ROW_TILES):
-            for j in range(EARLY_TILES):
-                multiply(j, rt)
-        for j in range(EARLY_TILES, SUM_BANKS):
-            if j == 3:
+        for j in range(SUM_BANKS):
+            multiply(j, 0)
+        for j in range(SUM_BANKS):
+            if j == SUM_BANKS - 1:
                 for rt in range(ROW_TILES):
                     nc.tensor.transpose(
                         row_term_all[:, rt * P : (rt + 1) * P],
                         row_term[:, rt : rt + 1].to_broadcast([P, P]),
                         ident_f32[:],
                     )
-            for rt in range(ROW_TILES):
-                multiply(j, rt)
+            multiply(j, 1)
 
         corrected = keep.tile([P, OUT_TILES, ROWS], F32)
         for j in range(OUT_TILES):

@@ -24,7 +24,7 @@ BANK_TILES = 4
 SUM_BANKS = 4
 HALVES = OUT_TILES // BANK_TILES
 C = 0.01 * 0.001 / 1
-EARLY_TILES = 3
+EARLY_TILES = 2
 
 FLOPS = 2 * ROWS * K * OUTS
 
@@ -66,8 +66,16 @@ def tile_optimalnet_pb_s_kernel(tc, vi, W_words, W_scales, b, out_0, out_1):
         warm(4)
 
         vi_sb = keep.tile([P, ROW_TILES, K], BF16)
-        for rt in range(ROW_TILES):
-            nc.scalar.dma_start(out=vi_sb[:, rt, :], in_=vi[rt * P : (rt + 1) * P, :])
+        nc.sync.dma_start(out=vi_sb[:, 0, :], in_=vi[0:P, :])
+        nc.scalar.dma_start(out=vi_sb[:, 1, :], in_=vi[P : 2 * P, :])
+        w_words = keep.tile([P, PASSES, 2 * OUTS], U8, align_bytes=64)
+        nc.sync.dma_start(
+            out=w_words[:].bitcast(I32), in_=W_words.bitcast(I32).rearrange("g p n -> p g n")
+        )
+
+        b_rows = keep.tile([P, P], BF16)
+        nc.vector.memset(b_rows[:], 0.0)
+        nc.sync.dma_start(out=b_rows[0:OUT_TILES, :], in_=b.rearrange("(j p) -> j p", p=P))
 
         w_scales = keep.tile([P, PASSES, OUTS], U8, align_bytes=64)
         nc.vector.memset(w_scales[:].bitcast(I32), 0)
@@ -75,16 +83,6 @@ def tile_optimalnet_pb_s_kernel(tc, vi, W_words, W_scales, b, out_0, out_1):
             nc.sync.dma_start(
                 out=w_scales[r:P:32, :, :].bitcast(I32),
                 in_=W_scales.bitcast(I32)[:, r:16:4, :].rearrange("g q n -> q g n"),
-            )
-        b_rows = keep.tile([P, P], BF16)
-        nc.vector.memset(b_rows[:], 0.0)
-        nc.sync.dma_start(out=b_rows[0:OUT_TILES, :], in_=b.rearrange("(j p) -> j p", p=P))
-        w_words = keep.tile([P, PASSES, 2 * OUTS], U8, align_bytes=64)
-        for h in range(HALVES):
-            word_bytes = slice(h * 2 * OUTS // HALVES, (h + 1) * 2 * OUTS // HALVES)
-            nc.sync.dma_start(
-                out=w_words[:, :, word_bytes].bitcast(I32),
-                in_=W_words[:, :, word_bytes].bitcast(I32).rearrange("g p n -> p g n"),
             )
 
         col_sum = keep.tile([P, P], F32)
@@ -118,7 +116,10 @@ def tile_optimalnet_pb_s_kernel(tc, vi, W_words, W_scales, b, out_0, out_1):
         for rt in range(ROW_TILES):
             vi_pairs = vi_sb[:, rt, :].bitcast(F32)
             for g in range(PASSES):
-                pairs_t = turned.tile([P, 2, P], F32, tag="turned")
+                if (rt, g) == (ROW_TILES - 1, PASSES - 1):
+                    pairs_t = sums.tile([P, 2, P], F32, tag="acc")
+                else:
+                    pairs_t = turned.tile([P, 2, P], F32, tag="turned")
                 pairs_of[(rt, g)] = pairs_t
                 for u in range(2):
                     nc.tensor.transpose(
@@ -132,7 +133,7 @@ def tile_optimalnet_pb_s_kernel(tc, vi, W_words, W_scales, b, out_0, out_1):
             for g in range(PASSES):
                 dst = grouped[:, rt, g, :].bitcast(F32).rearrange("p (r u) -> p r u", u=2)
                 src = pairs_of[(rt, g)][:].rearrange("p u r -> p r u")
-                if (rt, g) == (0, 0):
+                if g == 0:
                     nc.vector.tensor_copy(out=dst, in_=src)
                 else:
                     nc.scalar.copy(out=dst, in_=src)
@@ -151,9 +152,9 @@ def tile_optimalnet_pb_s_kernel(tc, vi, W_words, W_scales, b, out_0, out_1):
                 in_=grouped[:, rt, :, :].rearrange("p g c -> p (g c)"),
             )
 
+        warm(2)
         b_turned = turned.tile([P, P], BF16, tag="turned")
         nc.tensor.transpose(b_turned[:], b_rows[:], ident_bf16[:])
-        warm(2)
         b_col = keep.tile([P, OUT_TILES], F32)
         nc.vector.tensor_copy(out=b_col[:], in_=b_turned[:, 0:OUT_TILES])
 
@@ -177,17 +178,19 @@ def tile_optimalnet_pb_s_kernel(tc, vi, W_words, W_scales, b, out_0, out_1):
 
         for j in range(SUM_BANKS):
             open_sums(j)
-        for j in range(SUM_BANKS):
-            multiply(j, 0)
-        for j in range(SUM_BANKS):
-            if j == SUM_BANKS - 1:
+        for rt in range(ROW_TILES):
+            for j in range(EARLY_TILES):
+                multiply(j, rt)
+        for j in range(EARLY_TILES, SUM_BANKS):
+            for rt in range(ROW_TILES):
+                multiply(j, rt)
+            if j == EARLY_TILES:
                 for rt in range(ROW_TILES):
                     nc.tensor.transpose(
                         row_term_all[:, rt * P : (rt + 1) * P],
                         row_term[:, rt : rt + 1].to_broadcast([P, P]),
                         ident_f32[:],
                     )
-            multiply(j, 1)
 
         corrected = keep.tile([P, OUT_TILES, ROWS], F32)
         for j in range(OUT_TILES):

@@ -63,7 +63,7 @@ def tile_optimalnet_pb_s_kernel(tc, vi, W_words, W_scales, b, out_0, out_1):
             start=True,
             stop=True,
         )
-        warm(4)
+        warm(3)
 
         vi_sb = keep.tile([P, ROW_TILES, K], BF16)
         nc.sync.dma_start(out=vi_sb[:, 0, :], in_=vi[0:P, :])

@@ -20,11 +20,12 @@ ROWS, K, OUTS = 256, 1024, 1024
 ROW_TILES = ROWS // P
 PASSES = K // K_PASS
 OUT_TILES = OUTS // P
-BANK_TILES = 4
-SUM_BANKS = 4
-HALVES = OUT_TILES // BANK_TILES
+BANKS = 7
+GROUP = 2
+GROUPS = OUT_TILES // GROUP
 C = 0.01 * 0.001 / 1
-EARLY_TILES = 2
+AHEAD = 6
+EARLY_TILES = 3
 
 FLOPS = 2 * ROWS * K * OUTS
 
@@ -34,8 +35,8 @@ def tile_optimalnet_pb_s_kernel(tc, vi, W_words, W_scales, b, out_0, out_1):
     with ExitStack() as ctx:
         keep = ctx.enter_context(tc.tile_pool(name="keep", bufs=1))
         work = ctx.enter_context(tc.tile_pool(name="work", bufs=4))
-        turned = ctx.enter_context(tc.psum_pool(name="turned", bufs=3))
-        sums = ctx.enter_context(tc.psum_pool(name="sums", bufs=SUM_BANKS))
+        leaving = ctx.enter_context(tc.tile_pool(name="leaving", bufs=GROUPS + 1))
+        banks = ctx.enter_context(tc.psum_pool(name="banks", bufs=BANKS))
         spread = ctx.enter_context(tc.psum_pool(name="spread", bufs=1))
         ctx.enter_context(tc.manual_schedule())
 
@@ -69,13 +70,7 @@ def tile_optimalnet_pb_s_kernel(tc, vi, W_words, W_scales, b, out_0, out_1):
         nc.sync.dma_start(out=vi_sb[:, 0, :], in_=vi[0:P, :])
         nc.scalar.dma_start(out=vi_sb[:, 1, :], in_=vi[P : 2 * P, :])
         w_words = keep.tile([P, PASSES, 2 * OUTS], U8, align_bytes=64)
-        nc.sync.dma_start(
-            out=w_words[:].bitcast(I32), in_=W_words.bitcast(I32).rearrange("g p n -> p g n")
-        )
-
-        b_rows = keep.tile([P, P], BF16)
-        nc.vector.memset(b_rows[:], 0.0)
-        nc.sync.dma_start(out=b_rows[0:OUT_TILES, :], in_=b.rearrange("(j p) -> j p", p=P))
+        nc.sync.dma_start(out=w_words[:, 0, :].bitcast(I32), in_=W_words[0].bitcast(I32))
 
         w_scales = keep.tile([P, PASSES, OUTS], U8, align_bytes=64)
         nc.vector.memset(w_scales[:].bitcast(I32), 0)
@@ -84,11 +79,15 @@ def tile_optimalnet_pb_s_kernel(tc, vi, W_words, W_scales, b, out_0, out_1):
                 out=w_scales[r:P:32, :, :].bitcast(I32),
                 in_=W_scales.bitcast(I32)[:, r:16:4, :].rearrange("g q n -> q g n"),
             )
+        nc.sync.dma_start(out=w_words[:, 1, :].bitcast(I32), in_=W_words[1].bitcast(I32))
 
+        b_rows = keep.tile([P, P], BF16)
+        nc.vector.memset(b_rows[:], 0.0)
         col_sum = keep.tile([P, P], F32)
         nc.vector.memset(col_sum[:], 0.0)
         ident_f32 = keep.tile([P, P], F32)
         make_identity(nc, ident_f32[:])
+        nc.gpsimd.dma_start(out=b_rows[0:OUT_TILES, :], in_=b.rearrange("(j p) -> j p", p=P))
         ident_bf16 = keep.tile([P, P], BF16)
         make_identity(nc, ident_bf16[:])
 
@@ -112,14 +111,21 @@ def tile_optimalnet_pb_s_kernel(tc, vi, W_words, W_scales, b, out_0, out_1):
             out=row_term[:, 0:1], in0=row_sum[:], scalar1=C / ROWS, scalar2=None, op0=ALU.mult
         )
 
+        scaled = keep.tile([P, K], BF16)
+        part_mean = keep.tile([P, 1], F32)
+        nc.scalar.activation(
+            out=scaled[:, 0:K_PASS],
+            in_=vi_sb[:, 1, 0:K_PASS],
+            func=ACT.Copy,
+            scale=C / ROWS / K_PASS,
+            accum_out=part_mean[:],
+        )
+
         pairs_of = {}
         for rt in range(ROW_TILES):
             vi_pairs = vi_sb[:, rt, :].bitcast(F32)
             for g in range(PASSES):
-                if (rt, g) == (ROW_TILES - 1, PASSES - 1):
-                    pairs_t = sums.tile([P, 2, P], F32, tag="acc")
-                else:
-                    pairs_t = turned.tile([P, 2, P], F32, tag="turned")
+                pairs_t = banks.tile([P, 2, P], F32, tag="bank")
                 pairs_of[(rt, g)] = pairs_t
                 for u in range(2):
                     nc.tensor.transpose(
@@ -127,73 +133,66 @@ def tile_optimalnet_pb_s_kernel(tc, vi, W_words, W_scales, b, out_0, out_1):
                         vi_pairs[:, 256 * g + u : 256 * (g + 1) : 2],
                         ident_f32[:],
                     )
-            if rt == 0:
-                warm(0)
-        for rt in range(ROW_TILES):
-            for g in range(PASSES):
-                dst = grouped[:, rt, g, :].bitcast(F32).rearrange("p (r u) -> p r u", u=2)
-                src = pairs_of[(rt, g)][:].rearrange("p u r -> p r u")
-                if g == 0:
-                    nc.vector.tensor_copy(out=dst, in_=src)
-                else:
-                    nc.scalar.copy(out=dst, in_=src)
-        scaled = keep.tile([P, K], BF16)
-        nc.scalar.activation(
-            out=scaled[:],
-            in_=vi_sb[:, 1, :],
-            func=ACT.Copy,
-            scale=C / ROWS,
-            accum_out=row_term[:, 1:2],
-        )
-        for rt in range(ROW_TILES):
-            nc.vector.quantize_mx(
-                out=vi_codes[:, rt, :].bitcast(FP8X4),
-                scales=vi_scales[:, rt, :],
-                in_=grouped[:, rt, :, :].rearrange("p g c -> p (g c)"),
+
+        def spread_row_term(rt):
+            nc.tensor.transpose(
+                row_term_all[:, rt * P : (rt + 1) * P],
+                row_term[:, rt : rt + 1].to_broadcast([P, P]),
+                ident_f32[:],
             )
 
-        warm(2)
-        b_turned = turned.tile([P, P], BF16, tag="turned")
-        nc.tensor.transpose(b_turned[:], b_rows[:], ident_bf16[:])
-        b_col = keep.tile([P, OUT_TILES], F32)
-        nc.vector.tensor_copy(out=b_col[:], in_=b_turned[:, 0:OUT_TILES])
+        def interleave(rt, g, copy):
+            copy(
+                out=grouped[:, rt, g, :].bitcast(F32).rearrange("p (r u) -> p r u", u=2),
+                in_=pairs_of[(rt, g)][:].rearrange("p u r -> p r u"),
+            )
+
+        def quantise(rt, g):
+            nc.vector.quantize_mx(
+                out=vi_codes[:, rt, P * g : P * (g + 1)].bitcast(FP8X4),
+                scales=vi_scales[:, rt, P * g : P * (g + 1)],
+                in_=grouped[:, rt, g, :],
+            )
+
+        interleave(0, 0, nc.vector.tensor_copy)
+        interleave(0, 1, nc.scalar.copy)
+        quantise(0, 0)
+        interleave(1, 0, nc.vector.tensor_copy)
+        interleave(1, 1, nc.scalar.copy)
+        quantise(0, 1)
+        quantise(1, 0)
+        quantise(1, 1)
+        nc.scalar.activation(
+            out=scaled[:, K_PASS:K],
+            in_=vi_sb[:, 1, K_PASS:K],
+            func=ACT.Identity,
+            scale=C / ROWS,
+            bias=part_mean[:],
+            accum_out=row_term[:, 1:2],
+        )
 
         acc_of = {}
 
-        def open_sums(j):
-            acc = sums.tile([P, ROWS], F32, tag="acc")
-            acc_of[j] = acc
+        def one_pass(j, rt, g):
+            nc.tensor.matmul_mx(
+                out=acc_of[j][:, rt * P : (rt + 1) * P],
+                lhsT=w_words[:, g, 2 * P * j : 2 * P * (j + 1)].bitcast(FP4X4),
+                lhsT_scale=w_scales[:, g, P * j : P * (j + 1)],
+                rhs=vi_codes[:, rt, P * g : P * (g + 1)].bitcast(FP8X4),
+                rhs_scale=vi_scales[:, rt, P * g : P * (g + 1)],
+                start=(g == 0),
+                stop=(g == PASSES - 1),
+            )
 
         def multiply(j, rt):
             for g in range(PASSES):
-                nc.tensor.matmul_mx(
-                    out=acc_of[j][:, rt * P : (rt + 1) * P],
-                    lhsT=w_words[:, g, 2 * P * j : 2 * P * (j + 1)].bitcast(FP4X4),
-                    lhsT_scale=w_scales[:, g, P * j : P * (j + 1)],
-                    rhs=vi_codes[:, rt, P * g : P * (g + 1)].bitcast(FP8X4),
-                    rhs_scale=vi_scales[:, rt, P * g : P * (g + 1)],
-                    start=(g == 0),
-                    stop=(g == PASSES - 1),
-                )
+                one_pass(j, rt, g)
 
-        for j in range(SUM_BANKS):
-            open_sums(j)
-        for rt in range(ROW_TILES):
-            for j in range(EARLY_TILES):
-                multiply(j, rt)
-        for j in range(EARLY_TILES, SUM_BANKS):
-            for rt in range(ROW_TILES):
-                multiply(j, rt)
-            if j == EARLY_TILES:
-                for rt in range(ROW_TILES):
-                    nc.tensor.transpose(
-                        row_term_all[:, rt * P : (rt + 1) * P],
-                        row_term[:, rt : rt + 1].to_broadcast([P, P]),
-                        ident_f32[:],
-                    )
+        def open_sums(j):
+            acc = banks.tile([P, ROWS], F32, tag="bank")
+            acc_of[j] = acc
 
-        corrected = keep.tile([P, OUT_TILES, ROWS], F32)
-        for j in range(OUT_TILES):
+        def relu(j):
             vj = work.tile([P, ROWS], F32)
             nc.scalar.activation(
                 out=vj[:],
@@ -203,6 +202,11 @@ def tile_optimalnet_pb_s_kernel(tc, vi, W_words, W_scales, b, out_0, out_1):
                 scale=1.0,
                 accum_out=col_sum[:, j : j + 1],
             )
+            return vj
+
+        corrected = keep.tile([P, OUT_TILES, ROWS], F32)
+
+        def correct(j, vj):
             nc.vector.scalar_tensor_tensor(
                 out=corrected[:, j, :],
                 in0=row_term_all,
@@ -211,40 +215,90 @@ def tile_optimalnet_pb_s_kernel(tc, vi, W_words, W_scales, b, out_0, out_1):
                 op0=ALU.mult,
                 op1=ALU.add,
             )
-            if j + SUM_BANKS < OUT_TILES:
-                open_sums(j + SUM_BANKS)
-                for rt in range(ROW_TILES):
-                    multiply(j + SUM_BANKS, rt)
 
         back_of = {}
-        for h in range(HALVES):
-            for rt in range(ROW_TILES):
-                if (h, rt) == (HALVES - 1, ROW_TILES - 1):
-                    back = sums.tile([P, BANK_TILES * P], F32, tag="acc")
-                else:
-                    back = turned.tile([P, BANK_TILES * P], F32, tag="turned")
-                back_of[(h, rt)] = back
-        m_turned = sums.tile([P, P], F32, tag="acc")
-        for j in range(OUT_TILES):
-            if j == OUT_TILES - 1:
-                nc.tensor.transpose(m_turned[:], col_sum[:], ident_f32[:])
-            for rt in range(ROW_TILES):
-                nc.tensor.transpose(
-                    back_of[(j // BANK_TILES, rt)][:, (j % BANK_TILES) * P : (j % BANK_TILES + 1) * P],
-                    corrected[:, j, rt * P : (rt + 1) * P],
-                    ident_f32[:],
-                )
 
-        for h in range(HALVES):
+        def turn_back(q):
+            if q < GROUPS - 1:
+                back = banks.tile([P, ROW_TILES, GROUP * P], F32, tag="bank")
+                views = [back[:, rt, :] for rt in range(ROW_TILES)]
+            else:
+                views = []
+                for rt in range(ROW_TILES):
+                    half = banks.tile([P, GROUP * P], F32, tag="bank")
+                    views.append(half[:])
+            for i in range(GROUP):
+                j = GROUP * q + i
+                for rt in range(ROW_TILES):
+                    nc.tensor.transpose(
+                        views[rt][:, i * P : (i + 1) * P],
+                        corrected[:, j, rt * P : (rt + 1) * P],
+                        ident_f32[:],
+                    )
+            back_of[q] = back[:] if q < GROUPS - 1 else views
+
+        out_rows = out_0.rearrange("(t p) o -> p t o", p=P)
+
+        def leave(q, copy):
+            out_sb = leaving.tile([P, ROW_TILES, GROUP * P], F32)
+            copy(out=out_sb[:], in_=back_of[q])
+            nc.sync.dma_start(
+                out=out_rows[:, :, q * GROUP * P : (q + 1) * GROUP * P], in_=out_sb[:]
+            )
+
+        for j in range(EARLY_TILES):
+            open_sums(j)
+        for j in range(EARLY_TILES):
+            one_pass(j, 0, 0)
+        b_turned = banks.tile([P, P], BF16, tag="bank")
+        nc.tensor.transpose(b_turned[:], b_rows[:], ident_bf16[:])
+        b_col = keep.tile([P, OUT_TILES], F32)
+        nc.vector.tensor_copy(out=b_col[:], in_=b_turned[:, 0:OUT_TILES])
+        for j in range(EARLY_TILES):
+            one_pass(j, 0, 1)
+        for j in range(EARLY_TILES):
+            one_pass(j, 1, 0)
+        for j in range(EARLY_TILES):
+            one_pass(j, 1, 1)
+            if j == 0:
+                for rt in range(ROW_TILES):
+                    spread_row_term(rt)
+        for j in range(EARLY_TILES, AHEAD):
+            open_sums(j)
             for rt in range(ROW_TILES):
-                out_sb = work.tile([P, BANK_TILES * P], F32)
-                if rt == 0:
-                    nc.scalar.copy(out=out_sb[:], in_=back_of[(h, rt)][:])
-                else:
-                    nc.vector.tensor_copy(out=out_sb[:], in_=back_of[(h, rt)][:])
-                cols = slice(h * BANK_TILES * P, (h + 1) * BANK_TILES * P)
-                nc.sync.dma_start(out=out_0[rt * P : (rt + 1) * P, cols], in_=out_sb[:])
-            if h == 0:
-                m_rows = keep.tile([OUT_TILES, P], F32)
-                nc.scalar.mul(m_rows[:], m_turned[0:OUT_TILES, :], 1.0 / ROWS)
-                nc.sync.dma_start(out=out_1.rearrange("(j p) -> j p", p=P), in_=m_rows[:])
+                multiply(j, rt)
+
+        for j in range(OUT_TILES):
+            vj = relu(j)
+            correct(j, vj)
+            if j == 1:
+                turn_back(0)
+            if 1 <= j <= OUT_TILES - AHEAD:
+                open_sums(AHEAD + j - 1)
+                for rt in range(ROW_TILES):
+                    multiply(AHEAD + j - 1, rt)
+            if j == 3:
+                leave(0, nc.vector.tensor_copy)
+                turn_back(1)
+            if j == 5:
+                turn_back(2)
+        leave(1, nc.scalar.copy)
+        leave(2, nc.scalar.copy)
+        m_turned = banks.tile([P, P], F32, tag="bank")
+        nc.tensor.transpose(m_turned[:], col_sum[:], ident_f32[:])
+        m_rows = keep.tile([OUT_TILES, P], F32)
+        nc.vector.tensor_scalar(
+            out=m_rows[:],
+            in0=m_turned[0:OUT_TILES, :],
+            scalar1=1.0 / ROWS,
+            scalar2=None,
+            op0=ALU.mult,
+        )
+        nc.sync.dma_start(out=out_1.rearrange("(j p) -> j p", p=P), in_=m_rows[:])
+        turn_back(3)
+        for rt, copy in ((1, nc.vector.tensor_copy), (0, nc.scalar.copy)):
+            out_sb = leaving.tile([P, GROUP * P], F32)
+            copy(out=out_sb[:], in_=back_of[GROUPS - 1][rt])
+            nc.sync.dma_start(
+                out=out_0[rt * P : (rt + 1) * P, (GROUPS - 1) * GROUP * P :], in_=out_sb[:]
+            )

@@ -25,6 +25,7 @@ GROUP = 2
 GROUPS = OUT_TILES // GROUP
 C = 0.01 * 0.001 / 1
 AHEAD = 6
+LATE_WARM = 1
 EARLY_TILES = 3
 
 FLOPS = 2 * ROWS * K * OUTS
@@ -67,8 +68,11 @@ def tile_optimalnet_pb_s_kernel(tc, vi, W_words, W_scales, b, out_0, out_1):
         warm(3)
 
         vi_sb = keep.tile([P, ROW_TILES, K], BF16)
-        nc.sync.dma_start(out=vi_sb[:, 0, :], in_=vi[0:P, :])
-        nc.scalar.dma_start(out=vi_sb[:, 1, :], in_=vi[P : 2 * P, :])
+        for rt in range(ROW_TILES):
+            nc.sync.dma_start(out=vi_sb[:, rt, :], in_=vi[rt * P : (rt + 1) * P, :])
+        b_rows = keep.tile([P, P], BF16)
+        nc.vector.memset(b_rows[:], 0.0)
+        nc.scalar.dma_start(out=b_rows[0:OUT_TILES, :], in_=b.rearrange("(j p) -> j p", p=P))
         w_words = keep.tile([P, PASSES, 2 * OUTS], U8, align_bytes=64)
         nc.sync.dma_start(out=w_words[:, 0, :].bitcast(I32), in_=W_words[0].bitcast(I32))
 
@@ -81,13 +85,10 @@ def tile_optimalnet_pb_s_kernel(tc, vi, W_words, W_scales, b, out_0, out_1):
             )
         nc.sync.dma_start(out=w_words[:, 1, :].bitcast(I32), in_=W_words[1].bitcast(I32))
 
-        b_rows = keep.tile([P, P], BF16)
-        nc.vector.memset(b_rows[:], 0.0)
         col_sum = keep.tile([P, P], F32)
         nc.vector.memset(col_sum[:], 0.0)
         ident_f32 = keep.tile([P, P], F32)
         make_identity(nc, ident_f32[:])
-        nc.gpsimd.dma_start(out=b_rows[0:OUT_TILES, :], in_=b.rearrange("(j p) -> j p", p=P))
         ident_bf16 = keep.tile([P, P], BF16)
         make_identity(nc, ident_bf16[:])
 
@@ -134,6 +135,10 @@ def tile_optimalnet_pb_s_kernel(tc, vi, W_words, W_scales, b, out_0, out_1):
                         ident_f32[:],
                     )
 
+        b_turned = banks.tile([P, P], BF16, tag="bank")
+        nc.tensor.transpose(b_turned[:], b_rows[:], ident_bf16[:])
+        warm(LATE_WARM)
+
         def spread_row_term(rt):
             nc.tensor.transpose(
                 row_term_all[:, rt * P : (rt + 1) * P],
@@ -162,6 +167,8 @@ def tile_optimalnet_pb_s_kernel(tc, vi, W_words, W_scales, b, out_0, out_1):
         quantise(0, 1)
         quantise(1, 0)
         quantise(1, 1)
+        b_col = keep.tile([P, OUT_TILES], F32)
+        nc.vector.tensor_copy(out=b_col[:], in_=b_turned[:, 0:OUT_TILES])
         nc.scalar.activation(
             out=scaled[:, K_PASS:K],
             in_=vi_sb[:, 1, K_PASS:K],
@@ -250,10 +257,6 @@ def tile_optimalnet_pb_s_kernel(tc, vi, W_words, W_scales, b, out_0, out_1):
             open_sums(j)
         for j in range(EARLY_TILES):
             one_pass(j, 0, 0)
-        b_turned = banks.tile([P, P], BF16, tag="bank")
-        nc.tensor.transpose(b_turned[:], b_rows[:], ident_bf16[:])
-        b_col = keep.tile([P, OUT_TILES], F32)
-        nc.vector.tensor_copy(out=b_col[:], in_=b_turned[:, 0:OUT_TILES])
         for j in range(EARLY_TILES):
             one_pass(j, 0, 1)
         for j in range(EARLY_TILES):

@@ -72,9 +72,11 @@ def tile_optimalnet_pb_s_kernel(tc, vi, W_words, W_scales, b, out_0, out_1):
             nc.sync.dma_start(out=vi_sb[:, rt, :], in_=vi[rt * P : (rt + 1) * P, :])
         b_rows = keep.tile([P, P], BF16)
         nc.vector.memset(b_rows[:], 0.0)
-        nc.scalar.dma_start(out=b_rows[0:OUT_TILES, :], in_=b.rearrange("(j p) -> j p", p=P))
+        nc.sync.dma_start(out=b_rows[0:OUT_TILES, :], in_=b.rearrange("(j p) -> j p", p=P))
         w_words = keep.tile([P, PASSES, 2 * OUTS], U8, align_bytes=64)
-        nc.sync.dma_start(out=w_words[:, 0, :].bitcast(I32), in_=W_words[0].bitcast(I32))
+        nc.sync.dma_start(
+            out=w_words[:].bitcast(I32), in_=W_words.bitcast(I32).rearrange("g p n -> p g n")
+        )
 
         w_scales = keep.tile([P, PASSES, OUTS], U8, align_bytes=64)
         nc.vector.memset(w_scales[:].bitcast(I32), 0)
@@ -83,7 +85,6 @@ def tile_optimalnet_pb_s_kernel(tc, vi, W_words, W_scales, b, out_0, out_1):
                 out=w_scales[r:P:32, :, :].bitcast(I32),
                 in_=W_scales.bitcast(I32)[:, r:16:4, :].rearrange("g q n -> q g n"),
             )
-        nc.sync.dma_start(out=w_words[:, 1, :].bitcast(I32), in_=W_words[1].bitcast(I32))
 
         col_sum = keep.tile([P, P], F32)
         nc.vector.memset(col_sum[:], 0.0)

@@ -22,9 +22,7 @@ PASSES = K // K_PASS
 OUT_TILES = OUTS // P
 BANKS = 7
 GROUP = 2
-GROUPS = OUT_TILES // GROUP
 C = 0.01 * 0.001 / 1
-AHEAD = 6
 LATE_WARM = 1
 EARLY_TILES = 3
 
@@ -36,7 +34,6 @@ def tile_optimalnet_pb_s_kernel(tc, vi, W_words, W_scales, b, out_0, out_1):
     with ExitStack() as ctx:
         keep = ctx.enter_context(tc.tile_pool(name="keep", bufs=1))
         work = ctx.enter_context(tc.tile_pool(name="work", bufs=4))
-        leaving = ctx.enter_context(tc.tile_pool(name="leaving", bufs=GROUPS + 1))
         banks = ctx.enter_context(tc.psum_pool(name="banks", bufs=BANKS))
         spread = ctx.enter_context(tc.psum_pool(name="spread", bufs=1))
         ctx.enter_context(tc.manual_schedule())
@@ -71,12 +68,22 @@ def tile_optimalnet_pb_s_kernel(tc, vi, W_words, W_scales, b, out_0, out_1):
         for rt in range(ROW_TILES):
             nc.sync.dma_start(out=vi_sb[:, rt, :], in_=vi[rt * P : (rt + 1) * P, :])
         b_rows = keep.tile([P, P], BF16)
-        nc.vector.memset(b_rows[:], 0.0)
+        nc.gpsimd.memset(b_rows[:], 0.0)
         nc.sync.dma_start(out=b_rows[0:OUT_TILES, :], in_=b.rearrange("(j p) -> j p", p=P))
-        w_words = keep.tile([P, PASSES, 2 * OUTS], U8, align_bytes=64)
-        nc.sync.dma_start(
-            out=w_words[:].bitcast(I32), in_=W_words.bitcast(I32).rearrange("g p n -> p g n")
-        )
+        w_words = [
+            keep.tile([P, PASSES, OUTS], U8, align_bytes=64, name="w_words_%d" % half)
+            for half in range(2)
+        ]
+
+        def load_words(half):
+            nc.sync.dma_start(
+                out=w_words[half][:].bitcast(I32),
+                in_=W_words.bitcast(I32)[:, :, half * OUTS // 4 : (half + 1) * OUTS // 4].rearrange(
+                    "g p n -> p g n"
+                ),
+            )
+
+        load_words(0)
 
         w_scales = keep.tile([P, PASSES, OUTS], U8, align_bytes=64)
         nc.vector.memset(w_scales[:].bitcast(I32), 0)
@@ -85,6 +92,7 @@ def tile_optimalnet_pb_s_kernel(tc, vi, W_words, W_scales, b, out_0, out_1):
                 out=w_scales[r:P:32, :, :].bitcast(I32),
                 in_=W_scales.bitcast(I32)[:, r:16:4, :].rearrange("g q n -> q g n"),
             )
+        load_words(1)
 
         col_sum = keep.tile([P, P], F32)
         nc.vector.memset(col_sum[:], 0.0)
@@ -184,7 +192,7 @@ def tile_optimalnet_pb_s_kernel(tc, vi, W_words, W_scales, b, out_0, out_1):
         def one_pass(j, rt, g):
             nc.tensor.matmul_mx(
                 out=acc_of[j][:, rt * P : (rt + 1) * P],
-                lhsT=w_words[:, g, 2 * P * j : 2 * P * (j + 1)].bitcast(FP4X4),
+                lhsT=w_words[j // 4][:, g, 2 * P * (j % 4) : 2 * P * (j % 4 + 1)].bitcast(FP4X4),
                 lhsT_scale=w_scales[:, g, P * j : P * (j + 1)],
                 rhs=vi_codes[:, rt, P * g : P * (g + 1)].bitcast(FP8X4),
                 rhs_scale=vi_scales[:, rt, P * g : P * (g + 1)],
@@ -227,47 +235,35 @@ def tile_optimalnet_pb_s_kernel(tc, vi, W_words, W_scales, b, out_0, out_1):
         back_of = {}
 
         def turn_back(q):
-            if q < GROUPS - 1:
-                back = banks.tile([P, ROW_TILES, GROUP * P], F32, tag="bank")
-                views = [back[:, rt, :] for rt in range(ROW_TILES)]
-            else:
-                views = []
-                for rt in range(ROW_TILES):
-                    half = banks.tile([P, GROUP * P], F32, tag="bank")
-                    views.append(half[:])
+            for rt in range(ROW_TILES):
+                back = banks.tile([P, GROUP * P], F32, tag="bank")
+                back_of[(q, rt)] = back
             for i in range(GROUP):
-                j = GROUP * q + i
                 for rt in range(ROW_TILES):
                     nc.tensor.transpose(
-                        views[rt][:, i * P : (i + 1) * P],
-                        corrected[:, j, rt * P : (rt + 1) * P],
+                        back_of[(q, rt)][:, i * P : (i + 1) * P],
+                        corrected[:, GROUP * q + i, rt * P : (rt + 1) * P],
                         ident_f32[:],
                     )
-            back_of[q] = back[:] if q < GROUPS - 1 else views
 
-        out_rows = out_0.rearrange("(t p) o -> p t o", p=P)
+        out_sb = keep.tile([P, ROW_TILES, OUTS], F32)
 
-        def leave(q, copy):
-            out_sb = leaving.tile([P, ROW_TILES, GROUP * P], F32)
-            copy(out=out_sb[:], in_=back_of[q])
-            nc.sync.dma_start(
-                out=out_rows[:, :, q * GROUP * P : (q + 1) * GROUP * P], in_=out_sb[:]
-            )
+        def leave(q, rt):
+            cols = slice(q * GROUP * P, (q + 1) * GROUP * P)
+            copy = nc.scalar.copy if rt == 0 else nc.vector.tensor_copy
+            copy(out=out_sb[:, rt, cols], in_=back_of[(q, rt)][:])
+            nc.sync.dma_start(out=out_0[rt * P : (rt + 1) * P, cols], in_=out_sb[:, rt, cols])
 
         for j in range(EARLY_TILES):
             open_sums(j)
-        for j in range(EARLY_TILES):
-            one_pass(j, 0, 0)
-        for j in range(EARLY_TILES):
-            one_pass(j, 0, 1)
-        for j in range(EARLY_TILES):
-            one_pass(j, 1, 0)
-        for j in range(EARLY_TILES):
-            one_pass(j, 1, 1)
-            if j == 0:
-                for rt in range(ROW_TILES):
-                    spread_row_term(rt)
-        for j in range(EARLY_TILES, AHEAD):
+        for rt in range(ROW_TILES):
+            for g in range(PASSES):
+                for j in range(EARLY_TILES):
+                    one_pass(j, rt, g)
+                    if (rt, g, j) == (1, 1, 0):
+                        for half in range(ROW_TILES):
+                            spread_row_term(half)
+        for j in range(EARLY_TILES, OUT_TILES):
             open_sums(j)
             for rt in range(ROW_TILES):
                 multiply(j, rt)
@@ -275,19 +271,16 @@ def tile_optimalnet_pb_s_kernel(tc, vi, W_words, W_scales, b, out_0, out_1):
         for j in range(OUT_TILES):
             vj = relu(j)
             correct(j, vj)
-            if j == 1:
-                turn_back(0)
-            if 1 <= j <= OUT_TILES - AHEAD:
-                open_sums(AHEAD + j - 1)
-                for rt in range(ROW_TILES):
-                    multiply(AHEAD + j - 1, rt)
-            if j == 3:
-                leave(0, nc.vector.tensor_copy)
-                turn_back(1)
+            if j % GROUP == GROUP - 1:
+                turn_back(j // GROUP)
             if j == 5:
-                turn_back(2)
-        leave(1, nc.scalar.copy)
-        leave(2, nc.scalar.copy)
+                leave(0, 1)
+            if j == 6:
+                leave(0, 0)
+                leave(1, 1)
+        leave(1, 0)
+        leave(2, 0)
+        leave(2, 1)
         m_turned = banks.tile([P, P], F32, tag="bank")
         nc.tensor.transpose(m_turned[:], col_sum[:], ident_f32[:])
         m_rows = keep.tile([OUT_TILES, P], F32)
@@ -299,10 +292,5 @@ def tile_optimalnet_pb_s_kernel(tc, vi, W_words, W_scales, b, out_0, out_1):
             op0=ALU.mult,
         )
         nc.sync.dma_start(out=out_1.rearrange("(j p) -> j p", p=P), in_=m_rows[:])
-        turn_back(3)
-        for rt, copy in ((1, nc.vector.tensor_copy), (0, nc.scalar.copy)):
-            out_sb = leaving.tile([P, GROUP * P], F32)
-            copy(out=out_sb[:], in_=back_of[GROUPS - 1][rt])
-            nc.sync.dma_start(
-                out=out_0[rt * P : (rt + 1) * P, (GROUPS - 1) * GROUP * P :], in_=out_sb[:]
-            )
+        leave(3, 0)
+        leave(3, 1)

@@ -21,7 +21,8 @@ ROW_TILES = ROWS // P
 PASSES = K // K_PASS
 OUT_TILES = OUTS // P
 BANKS = 7
-GROUP = 2
+GROUPS = 4
+GROUP = OUT_TILES // GROUPS
 C = 0.01 * 0.001 / 1
 LATE_WARM = 1
 EARLY_TILES = 3
@@ -268,29 +269,19 @@ def tile_optimalnet_pb_s_kernel(tc, vi, W_words, W_scales, b, out_0, out_1):
             for rt in range(ROW_TILES):
                 multiply(j, rt)
 
+        def store_means():
+            m_turned = banks.tile([P, P], F32, tag="bank")
+            nc.tensor.transpose(m_turned[:], col_sum[:], ident_f32[:])
+            m_rows = keep.tile([OUT_TILES, P], F32)
+            nc.scalar.mul(m_rows[:], m_turned[0:OUT_TILES, :], 1.0 / ROWS)
+            nc.sync.dma_start(out=out_1.rearrange("(j p) -> j p", p=P), in_=m_rows[:])
+
         for j in range(OUT_TILES):
             vj = relu(j)
             correct(j, vj)
-            if j % GROUP == GROUP - 1:
-                turn_back(j // GROUP)
-            if j == 5:
-                leave(0, 1)
-            if j == 6:
-                leave(0, 0)
-                leave(1, 1)
-        leave(1, 0)
-        leave(2, 0)
-        leave(2, 1)
-        m_turned = banks.tile([P, P], F32, tag="bank")
-        nc.tensor.transpose(m_turned[:], col_sum[:], ident_f32[:])
-        m_rows = keep.tile([OUT_TILES, P], F32)
-        nc.vector.tensor_scalar(
-            out=m_rows[:],
-            in0=m_turned[0:OUT_TILES, :],
-            scalar1=1.0 / ROWS,
-            scalar2=None,
-            op0=ALU.mult,
-        )
-        nc.sync.dma_start(out=out_1.rearrange("(j p) -> j p", p=P), in_=m_rows[:])
-        leave(3, 0)
-        leave(3, 1)
+        for q in range(GROUPS):
+            if q == GROUPS - 1:
+                store_means()
+            turn_back(q)
+            for rt in range(ROW_TILES):
+                leave(q, rt)

@@ -253,7 +253,9 @@ def tile_optimalnet_pb_s_kernel(tc, vi, W_words, W_scales, b, out_0, out_1):
             cols = slice(q * GROUP * P, (q + 1) * GROUP * P)
             copy = nc.scalar.copy if rt == 0 else nc.vector.tensor_copy
             copy(out=out_sb[:, rt, cols], in_=back_of[(q, rt)][:])
-            nc.sync.dma_start(out=out_0[rt * P : (rt + 1) * P, cols], in_=out_sb[:, rt, cols])
+            if q % 2:
+                cols = slice((q - 1) * GROUP * P, (q + 1) * GROUP * P)
+                nc.sync.dma_start(out=out_0[rt * P : (rt + 1) * P, cols], in_=out_sb[:, rt, cols])
 
         for j in range(EARLY_TILES):
             open_sums(j)

@@ -21,11 +21,10 @@ ROW_TILES = ROWS // P
 PASSES = K // K_PASS
 OUT_TILES = OUTS // P
 BANKS = 7
-GROUPS = 4
-GROUP = OUT_TILES // GROUPS
 C = 0.01 * 0.001 / 1
 LATE_WARM = 1
-EARLY_TILES = 3
+VECTOR_RELU = 1
+EARLY_TILES = 4
 
 FLOPS = 2 * ROWS * K * OUTS
 
@@ -209,8 +208,21 @@ def tile_optimalnet_pb_s_kernel(tc, vi, W_words, W_scales, b, out_0, out_1):
             acc = banks.tile([P, ROWS], F32, tag="bank")
             acc_of[j] = acc
 
+        zeros = zero[:, 0:1].to_broadcast([P, ROWS])
+
         def relu(j):
             vj = work.tile([P, ROWS], F32)
+            if j == VECTOR_RELU:
+                nc.vector.scalar_tensor_tensor(
+                    out=vj[:],
+                    in0=acc_of[j][:],
+                    scalar=b_col[:, j : j + 1],
+                    in1=zeros,
+                    op0=ALU.add,
+                    op1=ALU.max,
+                    accum_out=col_sum[:, j : j + 1],
+                )
+                return vj
             nc.scalar.activation(
                 out=vj[:],
                 in_=acc_of[j][:],
@@ -235,26 +247,28 @@ def tile_optimalnet_pb_s_kernel(tc, vi, W_words, W_scales, b, out_0, out_1):
 
         back_of = {}
 
-        def turn_back(q):
+        def turn_back(tiles):
             for rt in range(ROW_TILES):
-                back = banks.tile([P, GROUP * P], F32, tag="bank")
-                back_of[(q, rt)] = back
-            for i in range(GROUP):
+                back = banks.tile([P, len(tiles) * P], F32, tag="bank")
+                back_of[rt] = back
+            for i, j in enumerate(tiles):
                 for rt in range(ROW_TILES):
                     nc.tensor.transpose(
-                        back_of[(q, rt)][:, i * P : (i + 1) * P],
-                        corrected[:, GROUP * q + i, rt * P : (rt + 1) * P],
+                        back_of[rt][:, i * P : (i + 1) * P],
+                        corrected[:, j, rt * P : (rt + 1) * P],
                         ident_f32[:],
                     )
 
         out_sb = keep.tile([P, ROW_TILES, OUTS], F32)
 
-        def leave(q, rt):
-            cols = slice(q * GROUP * P, (q + 1) * GROUP * P)
-            copy = nc.scalar.copy if rt == 0 else nc.vector.tensor_copy
-            copy(out=out_sb[:, rt, cols], in_=back_of[(q, rt)][:])
-            if q % 2:
-                cols = slice((q - 1) * GROUP * P, (q + 1) * GROUP * P)
+        def empty(tiles):
+            cols = slice(tiles[0] * P, (tiles[-1] + 1) * P)
+            nc.scalar.copy(out=out_sb[:, 0, cols], in_=back_of[0][:])
+            nc.vector.tensor_copy(out=out_sb[:, 1, cols], in_=back_of[1][:])
+
+        def store(h):
+            cols = slice(h * OUTS // 2, (h + 1) * OUTS // 2)
+            for rt in range(ROW_TILES):
                 nc.sync.dma_start(out=out_0[rt * P : (rt + 1) * P, cols], in_=out_sb[:, rt, cols])
 
         for j in range(EARLY_TILES):
@@ -263,7 +277,7 @@ def tile_optimalnet_pb_s_kernel(tc, vi, W_words, W_scales, b, out_0, out_1):
             for g in range(PASSES):
                 for j in range(EARLY_TILES):
                     one_pass(j, rt, g)
-                    if (rt, g, j) == (1, 1, 0):
+                    if (rt, g, j) == (1, 1, VECTOR_RELU):
                         for half in range(ROW_TILES):
                             spread_row_term(half)
         for j in range(EARLY_TILES, OUT_TILES):
@@ -278,12 +292,17 @@ def tile_optimalnet_pb_s_kernel(tc, vi, W_words, W_scales, b, out_0, out_1):
             nc.scalar.mul(m_rows[:], m_turned[0:OUT_TILES, :], 1.0 / ROWS)
             nc.sync.dma_start(out=out_1.rearrange("(j p) -> j p", p=P), in_=m_rows[:])
 
+        vj_of = {VECTOR_RELU: relu(VECTOR_RELU)}
         for j in range(OUT_TILES):
-            vj = relu(j)
-            correct(j, vj)
-        for q in range(GROUPS):
-            if q == GROUPS - 1:
-                store_means()
-            turn_back(q)
-            for rt in range(ROW_TILES):
-                leave(q, rt)
+            if j != VECTOR_RELU:
+                vj_of[j] = relu(j)
+            correct(j, vj_of[j])
+        turn_back((0, 1, 2, 3))
+        empty((0, 1, 2, 3))
+        store(0)
+        turn_back((4, 5))
+        empty((4, 5))
+        store_means()
+        turn_back((6, 7))
+        empty((6, 7))
+        store(1)

@@ -168,14 +168,10 @@ def tile_optimalnet_pb_s_kernel(tc, vi, W_words, W_scales, b, out_0, out_1):
                 in_=grouped[:, rt, g, :],
             )
 
-        interleave(0, 0, nc.vector.tensor_copy)
-        interleave(0, 1, nc.scalar.copy)
-        quantise(0, 0)
-        interleave(1, 0, nc.vector.tensor_copy)
-        interleave(1, 1, nc.scalar.copy)
-        quantise(0, 1)
-        quantise(1, 0)
-        quantise(1, 1)
+        for rt in range(ROW_TILES):
+            for g in range(PASSES):
+                interleave(rt, g, nc.vector.tensor_copy if (rt, g) == (0, 0) else nc.scalar.copy)
+                quantise(rt, g)
         b_col = keep.tile([P, OUT_TILES], F32)
         nc.vector.tensor_copy(out=b_col[:], in_=b_turned[:, 0:OUT_TILES])
         nc.scalar.activation(

@@ -24,6 +24,7 @@ BANKS = 7
 C = 0.01 * 0.001 / 1
 LATE_WARM = 1
 VECTOR_RELU = 1
+W_PARTS = ((0, 4), (4, 1), (5, 1), (6, 2))
 EARLY_TILES = 4
 
 FLOPS = 2 * ROWS * K * OUTS
@@ -70,18 +71,26 @@ def tile_optimalnet_pb_s_kernel(tc, vi, W_words, W_scales, b, out_0, out_1):
         b_rows = keep.tile([P, P], BF16)
         nc.gpsimd.memset(b_rows[:], 0.0)
         nc.sync.dma_start(out=b_rows[0:OUT_TILES, :], in_=b.rearrange("(j p) -> j p", p=P))
-        w_words = [
-            keep.tile([P, PASSES, OUTS], U8, align_bytes=64, name="w_words_%d" % half)
-            for half in range(2)
-        ]
-
-        def load_words(half):
-            nc.sync.dma_start(
-                out=w_words[half][:].bitcast(I32),
-                in_=W_words.bitcast(I32)[:, :, half * OUTS // 4 : (half + 1) * OUTS // 4].rearrange(
-                    "g p n -> p g n"
-                ),
+        w_words = []
+        for first, count in W_PARTS:
+            words = keep.tile(
+                [P, PASSES, 2 * P * count], U8, align_bytes=64, name="w_words_%d" % first
             )
+            w_words.append(words)
+
+        def load_words(part):
+            first, count = W_PARTS[part]
+            nc.sync.dma_start(
+                out=w_words[part][:].bitcast(I32),
+                in_=W_words.bitcast(I32)[
+                    :, :, first * P // 2 : (first + count) * P // 2
+                ].rearrange("g p n -> p g n"),
+            )
+
+        def words_of(j, g):
+            part = [n for n, (first, count) in enumerate(W_PARTS) if first <= j < first + count][0]
+            at = 2 * P * (j - W_PARTS[part][0])
+            return w_words[part][:, g, at : at + 2 * P].bitcast(FP4X4)
 
         load_words(0)
 
@@ -92,7 +101,8 @@ def tile_optimalnet_pb_s_kernel(tc, vi, W_words, W_scales, b, out_0, out_1):
                 out=w_scales[r:P:32, :, :].bitcast(I32),
                 in_=W_scales.bitcast(I32)[:, r:16:4, :].rearrange("g q n -> q g n"),
             )
-        load_words(1)
+        for part in range(1, len(W_PARTS)):
+            load_words(part)
 
         col_sum = keep.tile([P, P], F32)
         nc.vector.memset(col_sum[:], 0.0)
@@ -188,7 +198,7 @@ def tile_optimalnet_pb_s_kernel(tc, vi, W_words, W_scales, b, out_0, out_1):
         def one_pass(j, rt, g):
             nc.tensor.matmul_mx(
                 out=acc_of[j][:, rt * P : (rt + 1) * P],
-                lhsT=w_words[j // 4][:, g, 2 * P * (j % 4) : 2 * P * (j % 4 + 1)].bitcast(FP4X4),
+                lhsT=words_of(j, g),
                 lhsT_scale=w_scales[:, g, P * j : P * (j + 1)],
                 rhs=vi_codes[:, rt, P * g : P * (g + 1)].bitcast(FP8X4),
                 rhs_scale=vi_scales[:, rt, P * g : P * (g + 1)],

from contextlib import ExitStack

import concourse.mybir as mybir
from concourse.masks import make_identity

F32 = mybir.dt.float32
BF16 = mybir.dt.bfloat16
I32 = mybir.dt.int32
U32 = mybir.dt.uint32
U8 = mybir.dt.uint8
FP8X4 = mybir.dt.float8_e4m3fn_x4
FP4X4 = mybir.dt.float4_e2m1fn_x4
ACT = mybir.ActivationFunctionType
ALU = mybir.AluOpType

P = 128
PACK = 4
K_PASS = P * PACK
ROWS, K, OUTS = 256, 1024, 1024
ROW_TILES = ROWS // P
PASSES = K // K_PASS
OUT_TILES = OUTS // P
BANKS = 7
C = 0.01 * 0.001 / 1
LATE_WARM = 1
VECTOR_RELU = 1
W_PARTS = ((0, 4), (4, 1), (5, 1), (6, 2))
EARLY_TILES = 4

FLOPS = 2 * ROWS * K * OUTS


def tile_optimalnet_pb_s_kernel(tc, vi, W_words, W_scales, b, out_0, out_1):
    nc = tc.nc
    with ExitStack() as ctx:
        keep = ctx.enter_context(tc.tile_pool(name="keep", bufs=1))
        work = ctx.enter_context(tc.tile_pool(name="work", bufs=4))
        banks = ctx.enter_context(tc.psum_pool(name="banks", bufs=BANKS))
        spread = ctx.enter_context(tc.psum_pool(name="spread", bufs=1))
        ctx.enter_context(tc.manual_schedule())

        zero = keep.tile([P, 2], F32)
        nc.gpsimd.memset(zero[:], 0.0)
        spread_bank = spread.tile([P, 4 * P], F32)
        row_term_all = spread_bank[:, 0:ROWS]
        warm_out = spread_bank[:, ROWS : ROWS + P]

        def warm(passes):
            for i in range(passes):
                nc.tensor.matmul(
                    warm_out,
                    lhsT=zero[:, 0:1].to_broadcast([P, P]),
                    rhs=zero[:, 0:1].to_broadcast([P, P]),
                    start=True,
                    stop=True,
                )

        zero_bf16 = zero[:].bitcast(BF16)
        nc.tensor.matmul(
            spread_bank[:],
            lhsT=zero_bf16[:, 0:1].to_broadcast([P, P]),
            rhs=zero_bf16[:, 0:1].to_broadcast([P, 4 * P]),
            start=True,
            stop=True,
        )
        warm(3)

        vi_sb = keep.tile([P, ROW_TILES, K], BF16)
        for rt in range(ROW_TILES):
            nc.sync.dma_start(out=vi_sb[:, rt, :], in_=vi[rt * P : (rt + 1) * P, :])
        b_rows = keep.tile([P, P], BF16)
        nc.gpsimd.memset(b_rows[:], 0.0)
        nc.sync.dma_start(out=b_rows[0:OUT_TILES, :], in_=b.rearrange("(j p) -> j p", p=P))
        w_words = []
        for first, count in W_PARTS:
            words = keep.tile(
                [P, PASSES, 2 * P * count], U8, align_bytes=64, name="w_words_%d" % first
            )
            w_words.append(words)

        def load_words(part):
            first, count = W_PARTS[part]
            nc.sync.dma_start(
                out=w_words[part][:].bitcast(I32),
                in_=W_words.bitcast(I32)[
                    :, :, first * P // 2 : (first + count) * P // 2
                ].rearrange("g p n -> p g n"),
            )

        def words_of(j, g):
            part = [n for n, (first, count) in enumerate(W_PARTS) if first <= j < first + count][0]
            at = 2 * P * (j - W_PARTS[part][0])
            return w_words[part][:, g, at : at + 2 * P].bitcast(FP4X4)

        load_words(0)

        w_scales = keep.tile([P, PASSES, OUTS], U8, align_bytes=64)
        nc.vector.memset(w_scales[:].bitcast(I32), 0)
        for r in range(4):
            nc.sync.dma_start(
                out=w_scales[r:P:32, :, :].bitcast(I32),
                in_=W_scales.bitcast(I32)[:, r:16:4, :].rearrange("g q n -> q g n"),
            )
        for part in range(1, len(W_PARTS)):
            load_words(part)

        col_sum = keep.tile([P, P], F32)
        nc.vector.memset(col_sum[:], 0.0)
        ident_f32 = keep.tile([P, P], F32)
        make_identity(nc, ident_f32[:])
        ident_bf16 = keep.tile([P, P], BF16)
        make_identity(nc, ident_bf16[:])

        grouped = keep.tile([P, ROW_TILES, PASSES, P * PACK], BF16, align_bytes=64)
        vi_codes = keep.tile([P, ROW_TILES, PASSES * P], U32, align_bytes=64)
        vi_scales = keep.tile([P, ROW_TILES, PASSES * P], U8, align_bytes=64)
        row_term = keep.tile([P, ROW_TILES], F32)

        same = keep.tile([P, K], BF16)
        row_sum = keep.tile([P, 1], F32)
        nc.vector.tensor_scalar(
            out=same[:],
            in0=vi_sb[:, 0, :],
            scalar1=1.0,
            scalar2=None,
            op0=ALU.mult,
            op1=ALU.add,
            accum_out=row_sum[:],
        )
        nc.vector.tensor_scalar(
            out=row_term[:, 0:1], in0=row_sum[:], scalar1=C / ROWS, scalar2=None, op0=ALU.mult
        )

        scaled = keep.tile([P, K], BF16)
        part_mean = keep.tile([P, 1], F32)
        nc.scalar.activation(
            out=scaled[:, 0:K_PASS],
            in_=vi_sb[:, 1, 0:K_PASS],
            func=ACT.Copy,
            scale=C / ROWS / K_PASS,
            accum_out=part_mean[:],
        )

        pairs_of = {}
        for rt in range(ROW_TILES):
            vi_pairs = vi_sb[:, rt, :].bitcast(F32)
            for g in range(PASSES):
                pairs_t = banks.tile([P, 2, P], F32, tag="bank")
                pairs_of[(rt, g)] = pairs_t
                for u in range(2):
                    nc.tensor.transpose(
                        pairs_t[:, u, :],
                        vi_pairs[:, 256 * g + u : 256 * (g + 1) : 2],
                        ident_f32[:],
                    )

        b_turned = banks.tile([P, P], BF16, tag="bank")
        nc.tensor.transpose(b_turned[:], b_rows[:], ident_bf16[:])
        warm(LATE_WARM)

        def spread_row_term(rt):
            nc.tensor.transpose(
                row_term_all[:, rt * P : (rt + 1) * P],
                row_term[:, rt : rt + 1].to_broadcast([P, P]),
                ident_f32[:],
            )

        def interleave(rt, g, copy):
            copy(
                out=grouped[:, rt, g, :].bitcast(F32).rearrange("p (r u) -> p r u", u=2),
                in_=pairs_of[(rt, g)][:].rearrange("p u r -> p r u"),
            )

        def quantise(rt, g):
            nc.vector.quantize_mx(
                out=vi_codes[:, rt, P * g : P * (g + 1)].bitcast(FP8X4),
                scales=vi_scales[:, rt, P * g : P * (g + 1)],
                in_=grouped[:, rt, g, :],
            )

        for rt in range(ROW_TILES):
            for g in range(PASSES):
                interleave(rt, g, nc.vector.tensor_copy if (rt, g) == (0, 0) else nc.scalar.copy)
                quantise(rt, g)
        b_col = keep.tile([P, OUT_TILES], F32)
        nc.vector.tensor_copy(out=b_col[:], in_=b_turned[:, 0:OUT_TILES])
        nc.scalar.activation(
            out=scaled[:, K_PASS:K],
            in_=vi_sb[:, 1, K_PASS:K],
            func=ACT.Identity,
            scale=C / ROWS,
            bias=part_mean[:],
            accum_out=row_term[:, 1:2],
        )

        acc_of = {}

        def one_pass(j, rt, g):
            nc.tensor.matmul_mx(
                out=acc_of[j][:, rt * P : (rt + 1) * P],
                lhsT=words_of(j, g),
                lhsT_scale=w_scales[:, g, P * j : P * (j + 1)],
                rhs=vi_codes[:, rt, P * g : P * (g + 1)].bitcast(FP8X4),
                rhs_scale=vi_scales[:, rt, P * g : P * (g + 1)],
                start=(g == 0),
                stop=(g == PASSES - 1),
            )

        def multiply(j, rt):
            for g in range(PASSES):
                one_pass(j, rt, g)

        def open_sums(j):
            acc = banks.tile([P, ROWS], F32, tag="bank")
            acc_of[j] = acc

        zeros = zero[:, 0:1].to_broadcast([P, ROWS])

        def relu(j):
            vj = work.tile([P, ROWS], F32)
            if j == VECTOR_RELU:
                nc.vector.scalar_tensor_tensor(
                    out=vj[:],
                    in0=acc_of[j][:],
                    scalar=b_col[:, j : j + 1],
                    in1=zeros,
                    op0=ALU.add,
                    op1=ALU.max,
                    accum_out=col_sum[:, j : j + 1],
                )
                return vj
            nc.scalar.activation(
                out=vj[:],
                in_=acc_of[j][:],
                func=ACT.Relu,
                bias=b_col[:, j : j + 1],
                scale=1.0,
                accum_out=col_sum[:, j : j + 1],
            )
            return vj

        corrected = keep.tile([P, OUT_TILES, ROWS], F32)

        def correct(j, vj):
            nc.vector.scalar_tensor_tensor(
                out=corrected[:, j, :],
                in0=row_term_all,
                scalar=col_sum[:, j : j + 1],
                in1=vj[:],
                op0=ALU.mult,
                op1=ALU.add,
            )

        back_of = {}

        def turn_back(tiles):
            for rt in range(ROW_TILES):
                back = banks.tile([P, len(tiles) * P], F32, tag="bank")
                back_of[rt] = back
            for i, j in enumerate(tiles):
                for rt in range(ROW_TILES):
                    nc.tensor.transpose(
                        back_of[rt][:, i * P : (i + 1) * P],
                        corrected[:, j, rt * P : (rt + 1) * P],
                        ident_f32[:],
                    )

        out_sb = keep.tile([P, ROW_TILES, OUTS], F32)

        def empty(tiles):
            cols = slice(tiles[0] * P, (tiles[-1] + 1) * P)
            nc.scalar.copy(out=out_sb[:, 0, cols], in_=back_of[0][:])
            nc.vector.tensor_copy(out=out_sb[:, 1, cols], in_=back_of[1][:])

        def store(h):
            cols = slice(h * OUTS // 2, (h + 1) * OUTS // 2)
            for rt in range(ROW_TILES):
                nc.sync.dma_start(out=out_0[rt * P : (rt + 1) * P, cols], in_=out_sb[:, rt, cols])

        for j in range(EARLY_TILES):
            open_sums(j)
        for rt in range(ROW_TILES):
            for g in range(PASSES):
                for j in range(EARLY_TILES):
                    one_pass(j, rt, g)
                    if (rt, g, j) == (1, 1, VECTOR_RELU):
                        for half in range(ROW_TILES):
                            spread_row_term(half)
        for j in range(EARLY_TILES, OUT_TILES):
            open_sums(j)
            for rt in range(ROW_TILES):
                multiply(j, rt)

        def store_means():
            m_turned = banks.tile([P, P], F32, tag="bank")
            nc.tensor.transpose(m_turned[:], col_sum[:], ident_f32[:])
            m_rows = keep.tile([OUT_TILES, P], F32)
            nc.scalar.mul(m_rows[:], m_turned[0:OUT_TILES, :], 1.0 / ROWS)
            nc.sync.dma_start(out=out_1.rearrange("(j p) -> j p", p=P), in_=m_rows[:])

        vj_of = {VECTOR_RELU: relu(VECTOR_RELU)}
        for j in range(OUT_TILES):
            if j != VECTOR_RELU:
                vj_of[j] = relu(j)
            correct(j, vj_of[j])
        turn_back((0, 1, 2, 3))
        empty((0, 1, 2, 3))
        store(0)
        turn_back((4, 5))
        empty((4, 5))
        store_means()
        turn_back((6, 7))
        empty((6, 7))
        store(1)
